import numpy as np
import ml_dtypes


def mxq(x, axis, fmt="e4m3"):
    dtype, down = {"e4m3": (ml_dtypes.float8_e4m3fn, 7), "e5m2": (ml_dtypes.float8_e5m2, 14)}[fmt]
    v = np.moveaxis(np.asarray(x, np.float32).astype(ml_dtypes.bfloat16).astype(np.float64), axis, -1)
    blocks = v.reshape(v.shape[:-1] + (-1, 32))
    amax = np.abs(blocks).max(-1, keepdims=True)
    byte = np.maximum(np.where(amax > 0, np.frexp(amax)[1] - 1 + 127, 0) - down, 1)
    scale = np.exp2(byte - 127.0)
    codes = (blocks / scale).astype(np.float32).astype(dtype).astype(np.float64)
    return np.moveaxis((codes * scale).reshape(v.shape), -1, axis)


WIDE = False


def mx_kscale(k):
    if not WIDE:
        return np.ones(k)
    levels = np.array([10, -10, 5, -5, 0])
    a = np.random.permutation(np.resize(levels, k // 512 * 4)).reshape(k // 512, 4)
    idx = np.arange(k)
    return np.exp2(a[idx // 512, idx % 128 // 32])


BF16 = ml_dtypes.bfloat16


def bf(x):
    return np.asarray(x, np.float32).astype(BF16)


def f64(x):
    return np.asarray(x).astype(np.float64)


B, L, H = 2, 1024, 1024
HH = H // 2
BASE = 10000.0


def rope_tables():
    inv_freq = 1.0 / BASE ** (np.arange(0, H, 2) / H)
    freqs = np.outer(np.arange(L), inv_freq)
    emb = np.concatenate([freqs, freqs], axis=-1)
    return np.cos(emb), np.sin(emb)


def rotate_half(x):
    x1, x2 = np.split(x, 2, axis=-1)
    return np.concatenate([-x2, x1], axis=-1)


def setup_inputs():
    sh = mx_kscale(H)[:HH]
    s = np.concatenate([sh, sh])
    cos, sin = rope_tables()
    return {"hidden_states": bf(np.random.standard_normal((B, L, H)) * 0.2 * s),
            "W_q": bf(np.random.standard_normal((H, H)) * 0.5 / np.sqrt(H) / s[None, :]),
            "cos": bf(cos), "sin": bf(sin)}


def reference(hidden_states, W_q, cos, sin):
    x = f64(hidden_states)
    h = x * f64(cos)[None, :, :] + rotate_half(x) * f64(sin)[None, :, :]
    return mxq(h, 2, "e4m3") @ mxq(f64(W_q), 1, "e4m3").T

@@ -1,0 +1,218 @@
+from contextlib import ExitStack
+
+import concourse.mybir as mybir
+from concourse.masks import make_identity
+
+FLOPS = 2 * 2048 * 1024 * 1024
+
+F32 = mybir.dt.float32
+BF16 = mybir.dt.bfloat16
+U32 = mybir.dt.uint32
+U8 = mybir.dt.uint8
+FP8X4 = mybir.dt.float8_e4m3fn_x4
+MULT = mybir.AluOpType.mult
+
+P = 128
+B = 2
+H = 1024
+NT = 8
+CHUNKS = [(0, 1), (1, 2), (2, 4), (4, 6), (6, 8)]
+
+
+def tile_denseattentiononehead_pa_kernel(tc, hidden_states, W_q, cos, sin, out):
+    nc = tc.nc
+    xv = hidden_states.rearrange("b (q t) j -> q b t j", t=NT)
+    cv = cos.rearrange("(q t) j -> q t j", t=NT)
+    sv = sin.rearrange("(q t) j -> q t j", t=NT)
+    wv = W_q.rearrange("(t q) j -> q t j", q=P)
+    ov = out.rearrange("b (q t) o -> q b t o", t=NT)
+    with ExitStack() as ctx:
+        res = ctx.enter_context(tc.tile_pool(name="res", bufs=1))
+        prod = ctx.enter_context(tc.tile_pool(name="prod", bufs=3))
+        gpool = ctx.enter_context(tc.tile_pool(name="gpool", bufs=3))
+        opool = ctx.enter_context(tc.tile_pool(name="opool", bufs=3))
+        tp = ctx.enter_context(tc.psum_pool(name="tp", bufs=4))
+        pa = ctx.enter_context(tc.psum_pool(name="pa", bufs=4))
+        ctx.enter_context(tc.manual_schedule())
+
+        x_sb = res.tile([P, B, NT, H], BF16, name="x_sb")
+        cos_sb = res.tile([P, NT, H], BF16, name="cos_sb")
+        sin_sb = res.tile([P, NT, H], BF16, name="sin_sb")
+        w_sb = res.tile([P, NT, H], BF16, name="w_sb")
+        wg = res.tile([P, 2, 4 * H], BF16, name="wg", align_bytes=64)
+        wc = res.tile([P, 2, H], U32, name="wc", align_bytes=64)
+        ws = res.tile([P, 2, H], U8, name="ws", align_bytes=64)
+        hc = res.tile([P, NT, 512], U32, name="hc", align_bytes=64)
+        hs = res.tile([P, NT, 512], U8, name="hs", align_bytes=64)
+        ident = res.tile([P, P], F32, name="ident")
+
+        def load(c):
+            t0, t1 = CHUNKS[c]
+            nc.sync.dma_start(out=cos_sb[:, t0:t1, :], in_=cv[:, t0:t1, :])
+            nc.sync.dma_start(out=x_sb[:, :, t0:t1, :], in_=xv[:, :, t0:t1, :])
+            nc.sync.dma_start(out=sin_sb[:, t0:t1, 0:512], in_=sv[:, t0:t1, 512:1024])
+            nc.sync.dma_start(out=sin_sb[:, t0:t1, 512:1024], in_=sv[:, t0:t1, 0:512])
+
+        def load_w(a):
+            nc.sync.dma_start(out=w_sb[:, 4 * a:4 * a + 4, :], in_=wv[:, 4 * a:4 * a + 4, :])
+
+        load(0)
+        load_w(0)
+        load(1)
+        load_w(1)
+        load(2)
+        load(3)
+        load(4)
+        make_identity(nc, ident[:])
+
+        def negate(c):
+            t0, t1 = CHUNKS[c]
+            nc.vector.tensor_scalar_mul(
+                out=sin_sb[:, t0:t1, 512:1024], in0=sin_sb[:, t0:t1, 512:1024], scalar1=-1.0
+            )
+
+        def split(ap):
+            return ap.rearrange("q (k p e) -> q k e p", p=P, e=2)
+
+        tiles = {}
+
+        def mul(i, b):
+            if b == 0:
+                t1n = prod.tile([P, B, H], F32, name="t1", tag="t1")
+                t2n = prod.tile([P, B, H], F32, name="t2", tag="t2")
+                tiles[i] = (t1n, t2n)
+            t1, t2 = tiles[i]
+            xs = split(x_sb[:, b, i, :])
+            nc.vector.tensor_tensor(
+                out=t1[:, b, :].rearrange("q (k e p) -> q k e p", e=2, p=P),
+                in0=xs, in1=split(cos_sb[:, i, :]), op=MULT)
+            nc.vector.tensor_tensor(
+                out=t2[:, b, :].rearrange("q (k e p) -> q k e p", e=2, p=P),
+                in0=xs, in1=split(sin_sb[:, i, :]), op=MULT)
+
+        grps = {}
+
+        def tr(i, b):
+            if b == 0:
+                grpn = gpool.tile([P, B, 2, 512], BF16, name="grp", tag="grp", align_bytes=64)
+                grps[i] = grpn
+            grp = grps[i]
+            t1, t2 = tiles[i]
+            for g in range(2):
+                hb = tp.tile([P, 512], F32, name="hb", tag="tp")
+                for s in range(4):
+                    a = (4 * g + s) * P
+                    c = (4 * (1 - g) + s) * P
+                    nc.tensor.matmul(out=hb[:, s * P:(s + 1) * P], lhsT=t1[:, b, a:a + P],
+                                     rhs=ident[:], is_transpose=True, start=True, stop=False)
+                    nc.tensor.matmul(out=hb[:, s * P:(s + 1) * P], lhsT=t2[:, b, c:c + P],
+                                     rhs=ident[:], is_transpose=True, start=False, stop=True)
+                nc.scalar.copy(
+                    out=grp[:, b, g, :].rearrange("p (r s) -> p r s", s=4),
+                    in_=hb[:].rearrange("p (s r) -> p r s", s=4))
+
+        def quant(i):
+            nc.vector.quantize_mx(
+                out=hc[:, i, :].bitcast(FP8X4), scales=hs[:, i, :],
+                in_=grps[i][:].rearrange("p b g c -> p (b g c)"))
+
+        def quant_b(i, b):
+            nc.vector.quantize_mx(
+                out=hc[:, i, 256 * b:256 * b + 256].bitcast(FP8X4),
+                scales=hs[:, i, 256 * b:256 * b + 256],
+                in_=grps[i][:, b, :, :].rearrange("p g c -> p (g c)"))
+
+        def wtr(a):
+            for g in range(2):
+                for h in range(2):
+                    wb = tp.tile([P, 512], F32, name="wb", tag="tp")
+                    for u in range(2):
+                        for oi in range(2):
+                            src = w_sb[:, 4 * a + 2 * h + oi, :].bitcast(F32)
+                            nc.tensor.transpose(
+                                wb[:, u * 256 + oi * P:u * 256 + (oi + 1) * P],
+                                src[:, (2 * g + u) * P:(2 * g + u + 1) * P], ident[:])
+                    o0 = (512 * a + 256 * h) * 4
+                    nc.scalar.copy(
+                        out=wg[:, g, o0:o0 + 1024].bitcast(F32).rearrange("p (o u) -> p o u", u=2),
+                        in_=wb[:].rearrange("p (u o) -> p o u", u=2))
+
+        def wq(a):
+            for g in range(2):
+                nc.vector.quantize_mx(
+                    out=wc[:, g, 512 * a:512 * a + 512].bitcast(FP8X4),
+                    scales=ws[:, g, 512 * a:512 * a + 512],
+                    in_=wg[:, g, 2048 * a:2048 * a + 2048])
+
+        outs = {}
+
+        def mx(i, b, store_each=False):
+            if b == 0:
+                o_new = opool.tile([P, B, H], F32, name="o_sb", tag="o_sb")
+                outs[i] = o_new
+            o_sb = outs[i]
+            for nh in range(2):
+                acc = pa.tile([P, 512], F32, name="acc", tag="acc")
+                for g in range(2):
+                    m0 = (2 * b + g) * P
+                    nc.tensor.matmul_mx(
+                        out=acc[:],
+                        lhsT=hc[:, i, m0:m0 + P].bitcast(FP8X4),
+                        lhsT_scale=hs[:, i, m0:m0 + P],
+                        rhs=wc[:, g, 512 * nh:512 * nh + 512].bitcast(FP8X4),
+                        rhs_scale=ws[:, g, 512 * nh:512 * nh + 512],
+                        start=(g == 0), stop=(g == 1))
+                nc.scalar.copy(out=o_sb[:, b, 512 * nh:512 * nh + 512], in_=acc[:])
+            if store_each:
+                nc.sync.dma_start(out=ov[:, b, i, :], in_=o_sb[:, b, :])
+            elif b == 1:
+                nc.sync.dma_start(out=ov[:, :, i, :], in_=o_sb[:])
+
+        negate(0)
+        mul(0, 0)
+        tr(0, 0)
+        mul(0, 1)
+        tr(0, 1)
+        wtr(0)
+        negate(1)
+        mul(1, 0)
+        wq(0)
+        tr(1, 0)
+        mul(1, 1)
+        tr(1, 1)
+        quant(0)
+        wtr(1)
+        negate(2)
+        mul(2, 0)
+        wq(1)
+        tr(2, 0)
+        mx(0, 0)
+        mx(0, 1)
+        mul(2, 1)
+        tr(2, 1)
+        quant(1)
+        mx(1, 0)
+        mx(1, 1)
+        for i in range(3, 7):
+            if i == 4:
+                negate(3)
+            if i == 6:
+                negate(4)
+            mul(i, 0)
+            mul(i, 1)
+            tr(i, 0)
+            tr(i, 1)
+            quant(i - 1)
+            mx(i - 1, 0)
+            mx(i - 1, 1)
+        mul(7, 0)
+        quant(6)
+        tr(7, 0)
+        mx(6, 0)
+        mx(6, 1)
+        mul(7, 1)
+        quant_b(7, 0)
+        tr(7, 1)
+        mx(7, 0, True)
+        quant_b(7, 1)
+        mx(7, 1, True)

@@ -11,6 +11,8 @@ U32 = mybir.dt.uint32
 U8 = mybir.dt.uint8
 FP8X4 = mybir.dt.float8_e4m3fn_x4
 MULT = mybir.AluOpType.mult
+ADD = mybir.AluOpType.add
+SUB = mybir.AluOpType.subtract
 
 P = 128
 B = 2
@@ -29,13 +31,16 @@ def tile_denseattentiononehead_pa_kernel(tc, hidden_states, W_q, cos, sin, out):
     with ExitStack() as ctx:
         res = ctx.enter_context(tc.tile_pool(name="res", bufs=1))
         prod = ctx.enter_context(tc.tile_pool(name="prod", bufs=3))
+        tabs = ctx.enter_context(tc.tile_pool(name="tabs", bufs=2))
         gpool = ctx.enter_context(tc.tile_pool(name="gpool", bufs=3))
         opool = ctx.enter_context(tc.tile_pool(name="opool", bufs=3))
-        tp = ctx.enter_context(tc.psum_pool(name="tp", bufs=4))
-        pa = ctx.enter_context(tc.psum_pool(name="pa", bufs=4))
+        tp = ctx.enter_context(tc.psum_pool(name="tp", bufs=5))
+        pa = ctx.enter_context(tc.psum_pool(name="pa", bufs=3))
         ctx.enter_context(tc.manual_schedule())
 
-        x_sb = res.tile([P, B, NT, H], BF16, name="x_sb")
+        x0_sb = res.tile([P, NT, H], BF16, name="x0_sb")
+        x1_sb = res.tile([P, NT, H], BF16, name="x1_sb")
+        x_sb = [x0_sb, x1_sb]
         cos_sb = res.tile([P, NT, H], BF16, name="cos_sb")
         sin_sb = res.tile([P, NT, H], BF16, name="sin_sb")
         w_sb = res.tile([P, NT, H], BF16, name="w_sb")
@@ -49,13 +54,14 @@ def tile_denseattentiononehead_pa_kernel(tc, hidden_states, W_q, cos, sin, out):
         def load(c):
             t0, t1 = CHUNKS[c]
             nc.sync.dma_start(out=cos_sb[:, t0:t1, :], in_=cv[:, t0:t1, :])
-            nc.sync.dma_start(out=x_sb[:, :, t0:t1, :], in_=xv[:, :, t0:t1, :])
-            nc.sync.dma_start(out=sin_sb[:, t0:t1, 0:512], in_=sv[:, t0:t1, 512:1024])
-            nc.sync.dma_start(out=sin_sb[:, t0:t1, 512:1024], in_=sv[:, t0:t1, 0:512])
+            nc.sync.dma_start(out=sin_sb[:, t0:t1, :], in_=sv[:, t0:t1, :])
+            nc.sync.dma_start(out=x_sb[0][:, t0:t1, :], in_=xv[:, 0, t0:t1, :])
+            nc.sync.dma_start(out=x_sb[1][:, t0:t1, :], in_=xv[:, 1, t0:t1, :])
 
         def load_w(a):
             nc.sync.dma_start(out=w_sb[:, 4 * a:4 * a + 4, :], in_=wv[:, 4 * a:4 * a + 4, :])
 
+        make_identity(nc, ident[:])
         load(0)
         load_w(0)
         load(1)
@@ -63,18 +69,43 @@ def tile_denseattentiononehead_pa_kernel(tc, hidden_states, W_q, cos, sin, out):
         load(2)
         load(3)
         load(4)
-        make_identity(nc, ident[:])
 
-        def negate(c):
-            t0, t1 = CHUNKS[c]
-            nc.vector.tensor_scalar_mul(
-                out=sin_sb[:, t0:t1, 512:1024], in0=sin_sb[:, t0:t1, 512:1024], scalar1=-1.0
-            )
+        def word_t(dst, src, swap):
+            for u in range(2):
+                for g in range(2):
+                    w = 2 * ((1 - g) if swap else g) + u
+                    nc.tensor.transpose(dst[:, (2 * u + g) * P:(2 * u + g + 1) * P],
+                                        src[:, w * P:(w + 1) * P], ident[:])
 
-        def split(ap):
-            return ap.rearrange("q (k p e) -> q k e p", p=P, e=2)
+        def pairs_out(dst_bf16, bank):
+            nc.scalar.copy(
+                out=dst_bf16.bitcast(F32).rearrange("p (r u) -> p r u", u=2),
+                in_=bank[:].rearrange("p (u r) -> p r u", u=2))
 
+        tab = {}
+        xbs = {}
         tiles = {}
+        grps = {}
+        outs = {}
+
+        def tab_t(i):
+            cb = tp.tile([P, 512], F32, name="cb", tag="tp")
+            word_t(cb, cos_sb[:, i, :].bitcast(F32), False)
+            cos_t = tabs.tile([P, H], BF16, name="cos_t", tag="cos_t")
+            pairs_out(cos_t[:], cb)
+            sb = tp.tile([P, 512], F32, name="sb", tag="tp")
+            word_t(sb, sin_sb[:, i, :].bitcast(F32), True)
+            sin_t = tabs.tile([P, H], BF16, name="sin_t", tag="sin_t")
+            pairs_out(sin_t[:], sb)
+            tab[i] = (cos_t, sin_t)
+
+        def x_t(i, b):
+            xb = tp.tile([P, 512], F32, name="xb", tag="tp")
+            word_t(xb, x_sb[b][:, i, :].bitcast(F32), False)
+            xbs[(i, b)] = xb
+
+        def rue(ap):
+            return ap.rearrange("p (r u e) -> p r u e", u=2, e=2)
 
         def mul(i, b):
             if b == 0:
@@ -82,45 +113,22 @@ def tile_denseattentiononehead_pa_kernel(tc, hidden_states, W_q, cos, sin, out):
                 t2n = prod.tile([P, B, H], F32, name="t2", tag="t2")
                 tiles[i] = (t1n, t2n)
             t1, t2 = tiles[i]
-            xs = split(x_sb[:, b, i, :])
-            nc.vector.tensor_tensor(
-                out=t1[:, b, :].rearrange("q (k e p) -> q k e p", e=2, p=P),
-                in0=xs, in1=split(cos_sb[:, i, :]), op=MULT)
-            nc.vector.tensor_tensor(
-                out=t2[:, b, :].rearrange("q (k e p) -> q k e p", e=2, p=P),
-                in0=xs, in1=split(sin_sb[:, i, :]), op=MULT)
+            cos_t, sin_t = tab[i]
+            xin = xbs[(i, b)][:].bitcast(BF16).rearrange("p (u r e) -> p r u e", u=2, e=2)
+            nc.vector.tensor_tensor(out=rue(t1[:, b, :]), in0=xin, in1=rue(cos_t[:]), op=MULT)
+            nc.vector.tensor_tensor(out=rue(t2[:, b, :]), in0=xin, in1=rue(sin_t[:]), op=MULT)
 
-        grps = {}
-
-        def tr(i, b):
-            if b == 0:
-                grpn = gpool.tile([P, B, 2, 512], BF16, name="grp", tag="grp", align_bytes=64)
-                grps[i] = grpn
-            grp = grps[i]
+        def add(i, eng):
+            grpn = gpool.tile([P, B, 2, 512], BF16, name="grp", tag="grp", align_bytes=64)
+            grps[i] = grpn
             t1, t2 = tiles[i]
-            for g in range(2):
-                hb = tp.tile([P, 512], F32, name="hb", tag="tp")
-                for s in range(4):
-                    a = (4 * g + s) * P
-                    c = (4 * (1 - g) + s) * P
-                    nc.tensor.matmul(out=hb[:, s * P:(s + 1) * P], lhsT=t1[:, b, a:a + P],
-                                     rhs=ident[:], is_transpose=True, start=True, stop=False)
-                    nc.tensor.matmul(out=hb[:, s * P:(s + 1) * P], lhsT=t2[:, b, c:c + P],
-                                     rhs=ident[:], is_transpose=True, start=False, stop=True)
-                nc.scalar.copy(
-                    out=grp[:, b, g, :].rearrange("p (r s) -> p r s", s=4),
-                    in_=hb[:].rearrange("p (s r) -> p r s", s=4))
+            eng.tensor_tensor(out=grpn[:, :, 0, :], in0=t1[:, :, 0:512], in1=t2[:, :, 512:1024], op=SUB)
+            eng.tensor_tensor(out=grpn[:, :, 1, :], in0=t1[:, :, 512:1024], in1=t2[:, :, 0:512], op=ADD)
 
         def quant(i):
             nc.vector.quantize_mx(
                 out=hc[:, i, :].bitcast(FP8X4), scales=hs[:, i, :],
                 in_=grps[i][:].rearrange("p b g c -> p (b g c)"))
-
-        def quant_b(i, b):
-            nc.vector.quantize_mx(
-                out=hc[:, i, 256 * b:256 * b + 256].bitcast(FP8X4),
-                scales=hs[:, i, 256 * b:256 * b + 256],
-                in_=grps[i][:, b, :, :].rearrange("p g c -> p (g c)"))
 
         def wtr(a):
             for g in range(2):
@@ -133,9 +141,7 @@ def tile_denseattentiononehead_pa_kernel(tc, hidden_states, W_q, cos, sin, out):
                                 wb[:, u * 256 + oi * P:u * 256 + (oi + 1) * P],
                                 src[:, (2 * g + u) * P:(2 * g + u + 1) * P], ident[:])
                     o0 = (512 * a + 256 * h) * 4
-                    nc.scalar.copy(
-                        out=wg[:, g, o0:o0 + 1024].bitcast(F32).rearrange("p (o u) -> p o u", u=2),
-                        in_=wb[:].rearrange("p (u o) -> p o u", u=2))
+                    pairs_out(wg[:, g, o0:o0 + 1024], wb)
 
         def wq(a):
             for g in range(2):
@@ -144,9 +150,7 @@ def tile_denseattentiononehead_pa_kernel(tc, hidden_states, W_q, cos, sin, out):
                     scales=ws[:, g, 512 * a:512 * a + 512],
                     in_=wg[:, g, 2048 * a:2048 * a + 2048])
 
-        outs = {}
-
-        def mx(i, b, store_each=False):
+        def mx(i, b):
             if b == 0:
                 o_new = opool.tile([P, B, H], F32, name="o_sb", tag="o_sb")
                 outs[i] = o_new
@@ -163,56 +167,33 @@ def tile_denseattentiononehead_pa_kernel(tc, hidden_states, W_q, cos, sin, out):
                         rhs_scale=ws[:, g, 512 * nh:512 * nh + 512],
                         start=(g == 0), stop=(g == 1))
                 nc.scalar.copy(out=o_sb[:, b, 512 * nh:512 * nh + 512], in_=acc[:])
-            if store_each:
-                nc.sync.dma_start(out=ov[:, b, i, :], in_=o_sb[:, b, :])
-            elif b == 1:
+            if b == 1:
                 nc.sync.dma_start(out=ov[:, :, i, :], in_=o_sb[:])
 
-        negate(0)
-        mul(0, 0)
-        tr(0, 0)
-        mul(0, 1)
-        tr(0, 1)
-        wtr(0)
-        negate(1)
-        mul(1, 0)
-        wq(0)
-        tr(1, 0)
-        mul(1, 1)
-        tr(1, 1)
-        quant(0)
-        wtr(1)
-        negate(2)
-        mul(2, 0)
-        wq(1)
-        tr(2, 0)
-        mx(0, 0)
-        mx(0, 1)
-        mul(2, 1)
-        tr(2, 1)
-        quant(1)
-        mx(1, 0)
-        mx(1, 1)
-        for i in range(3, 7):
-            if i == 4:
-                negate(3)
-            if i == 6:
-                negate(4)
-            mul(i, 0)
-            mul(i, 1)
-            tr(i, 0)
-            tr(i, 1)
-            quant(i - 1)
-            mx(i - 1, 0)
-            mx(i - 1, 1)
-        mul(7, 0)
-        quant(6)
-        tr(7, 0)
-        mx(6, 0)
-        mx(6, 1)
-        mul(7, 1)
-        quant_b(7, 0)
-        tr(7, 1)
-        mx(7, 0, True)
-        quant_b(7, 1)
-        mx(7, 1, True)
+        tab_t(0)
+        x_t(0, 0)
+        x_t(0, 1)
+        for i in range(NT + 2):
+            if i < NT:
+                mul(i, 0)
+            if i == 1:
+                wq(0)
+            if i == 2:
+                wq(1)
+            if i >= 2:
+                quant(i - 2)
+            if i < NT:
+                mul(i, 1)
+            if i == 0:
+                wtr(0)
+            if i + 1 < NT:
+                tab_t(i + 1)
+                x_t(i + 1, 0)
+                x_t(i + 1, 1)
+            if i == 1:
+                wtr(1)
+            if i < NT:
+                add(i, nc.gpsimd)
+            if i >= 2:
+                mx(i - 2, 0)
+                mx(i - 2, 1)

@@ -18,7 +18,7 @@ P = 128
 B = 2
 H = 1024
 NT = 8
-CHUNKS = [(0, 1), (1, 2), (2, 4), (4, 6), (6, 8)]
+CHUNKS = [(0, 1), (1, 2), (2, 3), (3, 4), (4, 6), (6, 8)]
 
 
 def tile_denseattentiononehead_pa_kernel(tc, hidden_states, W_q, cos, sin, out):
@@ -32,10 +32,11 @@ def tile_denseattentiononehead_pa_kernel(tc, hidden_states, W_q, cos, sin, out):
         res = ctx.enter_context(tc.tile_pool(name="res", bufs=1))
         prod = ctx.enter_context(tc.tile_pool(name="prod", bufs=3))
         tabs = ctx.enter_context(tc.tile_pool(name="tabs", bufs=2))
-        gpool = ctx.enter_context(tc.tile_pool(name="gpool", bufs=3))
+        gpool = ctx.enter_context(tc.tile_pool(name="gpool", bufs=1))
         opool = ctx.enter_context(tc.tile_pool(name="opool", bufs=3))
-        tp = ctx.enter_context(tc.psum_pool(name="tp", bufs=5))
-        pa = ctx.enter_context(tc.psum_pool(name="pa", bufs=3))
+        px = ctx.enter_context(tc.psum_pool(name="px", bufs=4))
+        tp = ctx.enter_context(tc.psum_pool(name="tp", bufs=2))
+        pa = ctx.enter_context(tc.psum_pool(name="pa", bufs=2))
         ctx.enter_context(tc.manual_schedule())
 
         x0_sb = res.tile([P, NT, H], BF16, name="x0_sb")
@@ -54,8 +55,8 @@ def tile_denseattentiononehead_pa_kernel(tc, hidden_states, W_q, cos, sin, out):
         def load(c):
             t0, t1 = CHUNKS[c]
             nc.sync.dma_start(out=cos_sb[:, t0:t1, :], in_=cv[:, t0:t1, :])
-            nc.sync.dma_start(out=sin_sb[:, t0:t1, :], in_=sv[:, t0:t1, :])
             nc.sync.dma_start(out=x_sb[0][:, t0:t1, :], in_=xv[:, 0, t0:t1, :])
+            nc.sync.dma_start(out=sin_sb[:, t0:t1, :], in_=sv[:, t0:t1, :])
             nc.sync.dma_start(out=x_sb[1][:, t0:t1, :], in_=xv[:, 1, t0:t1, :])
 
         def load_w(a):
@@ -63,12 +64,13 @@ def tile_denseattentiononehead_pa_kernel(tc, hidden_states, W_q, cos, sin, out):
 
         make_identity(nc, ident[:])
         load(0)
-        load_w(0)
         load(1)
-        load_w(1)
+        load_w(0)
         load(2)
+        load_w(1)
         load(3)
         load(4)
+        load(5)
 
         def word_t(dst, src, swap):
             for u in range(2):
@@ -88,19 +90,22 @@ def tile_denseattentiononehead_pa_kernel(tc, hidden_states, W_q, cos, sin, out):
         grps = {}
         outs = {}
 
-        def tab_t(i):
+        def cos_tr(i):
             cb = tp.tile([P, 512], F32, name="cb", tag="tp")
             word_t(cb, cos_sb[:, i, :].bitcast(F32), False)
             cos_t = tabs.tile([P, H], BF16, name="cos_t", tag="cos_t")
             pairs_out(cos_t[:], cb)
+            tab[(i, 0)] = cos_t
+
+        def sin_tr(i):
             sb = tp.tile([P, 512], F32, name="sb", tag="tp")
             word_t(sb, sin_sb[:, i, :].bitcast(F32), True)
             sin_t = tabs.tile([P, H], BF16, name="sin_t", tag="sin_t")
             pairs_out(sin_t[:], sb)
-            tab[i] = (cos_t, sin_t)
+            tab[(i, 1)] = sin_t
 
         def x_t(i, b):
-            xb = tp.tile([P, 512], F32, name="xb", tag="tp")
+            xb = px.tile([P, 512], F32, name="xb", tag="xb")
             word_t(xb, x_sb[b][:, i, :].bitcast(F32), False)
             xbs[(i, b)] = xb
 
@@ -113,17 +118,36 @@ def tile_denseattentiononehead_pa_kernel(tc, hidden_states, W_q, cos, sin, out):
                 t2n = prod.tile([P, B, H], F32, name="t2", tag="t2")
                 tiles[i] = (t1n, t2n)
             t1, t2 = tiles[i]
-            cos_t, sin_t = tab[i]
+            cos_t = tab[(i, 0)]
+            sin_t = tab[(i, 1)]
             xin = xbs[(i, b)][:].bitcast(BF16).rearrange("p (u r e) -> p r u e", u=2, e=2)
             nc.vector.tensor_tensor(out=rue(t1[:, b, :]), in0=xin, in1=rue(cos_t[:]), op=MULT)
             nc.vector.tensor_tensor(out=rue(t2[:, b, :]), in0=xin, in1=rue(sin_t[:]), op=MULT)
 
-        def add(i, eng):
-            grpn = gpool.tile([P, B, 2, 512], BF16, name="grp", tag="grp", align_bytes=64)
-            grps[i] = grpn
+        def grp_of(i):
+            if i not in grps:
+                grpn = gpool.tile([P, B, 2, 512], BF16, name="grp", tag="grp", align_bytes=64)
+                grps[i] = grpn
+            return grps[i]
+
+        def add_g(i, g, eng):
+            grp = grp_of(i)
             t1, t2 = tiles[i]
-            eng.tensor_tensor(out=grpn[:, :, 0, :], in0=t1[:, :, 0:512], in1=t2[:, :, 512:1024], op=SUB)
-            eng.tensor_tensor(out=grpn[:, :, 1, :], in0=t1[:, :, 512:1024], in1=t2[:, :, 0:512], op=ADD)
+            eng.tensor_tensor(out=grp[:, :, g, :], in0=t1[:, :, 512 * g:512 * g + 512],
+                              in1=t2[:, :, 512 * (1 - g):512 * (1 - g) + 512], op=(SUB if g == 0 else ADD))
+
+        def add_b(i, b, eng):
+            grp = grp_of(i)
+            t1, t2 = tiles[i]
+            for g in range(2):
+                eng.tensor_tensor(out=grp[:, b, g, :], in0=t1[:, b, 512 * g:512 * g + 512],
+                                  in1=t2[:, b, 512 * (1 - g):512 * (1 - g) + 512], op=(SUB if g == 0 else ADD))
+
+        def quant_b(i, b):
+            nc.vector.quantize_mx(
+                out=hc[:, i, 256 * b:256 * b + 256].bitcast(FP8X4),
+                scales=hs[:, i, 256 * b:256 * b + 256],
+                in_=grps[i][:, b, :, :].rearrange("p g c -> p (g c)"))
 
         def quant(i):
             nc.vector.quantize_mx(
@@ -150,7 +174,7 @@ def tile_denseattentiononehead_pa_kernel(tc, hidden_states, W_q, cos, sin, out):
                     scales=ws[:, g, 512 * a:512 * a + 512],
                     in_=wg[:, g, 2048 * a:2048 * a + 2048])
 
-        def mx(i, b):
+        def mx(i, b, last=False, both=False):
             if b == 0:
                 o_new = opool.tile([P, B, H], F32, name="o_sb", tag="o_sb")
                 outs[i] = o_new
@@ -166,34 +190,57 @@ def tile_denseattentiononehead_pa_kernel(tc, hidden_states, W_q, cos, sin, out):
                         rhs=wc[:, g, 512 * nh:512 * nh + 512].bitcast(FP8X4),
                         rhs_scale=ws[:, g, 512 * nh:512 * nh + 512],
                         start=(g == 0), stop=(g == 1))
-                nc.scalar.copy(out=o_sb[:, b, 512 * nh:512 * nh + 512], in_=acc[:])
-            if b == 1:
+                if both and nh == 1:
+                    nc.vector.tensor_copy(out=o_sb[:, b, 512 * nh:512 * nh + 512], in_=acc[:])
+                else:
+                    nc.scalar.copy(out=o_sb[:, b, 512 * nh:512 * nh + 512], in_=acc[:])
+            if last:
+                nc.sync.dma_start(out=ov[:, b, i, :], in_=o_sb[:, b, :])
+            elif b == 1:
                 nc.sync.dma_start(out=ov[:, :, i, :], in_=o_sb[:])
 
-        tab_t(0)
-        x_t(0, 0)
-        x_t(0, 1)
-        for i in range(NT + 2):
-            if i < NT:
-                mul(i, 0)
+        def t_all(i):
+            cos_tr(i)
+            x_t(i, 0)
+            sin_tr(i)
+            x_t(i, 1)
+
+        t_all(0)
+        t_all(1)
+        for i in range(7):
+            mul(i, 0)
+            if i == 0:
+                add_b(0, 0, nc.gpsimd)
+            mul(i, 1)
+            if i < 2:
+                wtr(i)
+            if i + 2 < NT:
+                t_all(i + 2)
             if i == 1:
                 wq(0)
             if i == 2:
                 wq(1)
-            if i >= 2:
-                quant(i - 2)
-            if i < NT:
-                mul(i, 1)
+            if i >= 1:
+                quant(i - 1)
             if i == 0:
-                wtr(0)
-            if i + 1 < NT:
-                tab_t(i + 1)
-                x_t(i + 1, 0)
-                x_t(i + 1, 1)
-            if i == 1:
-                wtr(1)
-            if i < NT:
-                add(i, nc.gpsimd)
+                add_b(0, 1, nc.gpsimd)
+            else:
+                add_g(i, 0, nc.gpsimd)
+                add_g(i, 1, nc.vector if i == 6 else nc.gpsimd)
+            if i == 2:
+                mx(0, 0)
+                mx(0, 1)
             if i >= 2:
-                mx(i - 2, 0)
-                mx(i - 2, 1)
+                mx(i - 1, 0)
+                mx(i - 1, 1)
+        mul(7, 0)
+        quant(6)
+        add_b(7, 0, nc.gpsimd)
+        mx(6, 0)
+        mx(6, 1)
+        mul(7, 1)
+        quant_b(7, 0)
+        mx(7, 0, True)
+        add_b(7, 1, nc.vector)
+        quant_b(7, 1)
+        mx(7, 1, True, True)

@@ -136,6 +136,12 @@ def tile_denseattentiononehead_pa_kernel(tc, hidden_states, W_q, cos, sin, out):
             eng.tensor_tensor(out=grp[:, :, g, :], in0=t1[:, :, 512 * g:512 * g + 512],
                               in1=t2[:, :, 512 * (1 - g):512 * (1 - g) + 512], op=(SUB if g == 0 else ADD))
 
+        def add_p(i, b, g, eng):
+            grp = grp_of(i)
+            t1, t2 = tiles[i]
+            eng.tensor_tensor(out=grp[:, b, g, :], in0=t1[:, b, 512 * g:512 * g + 512],
+                              in1=t2[:, b, 512 * (1 - g):512 * (1 - g) + 512], op=(SUB if g == 0 else ADD))
+
         def add_b(i, b, eng):
             grp = grp_of(i)
             t1, t2 = tiles[i]
@@ -220,13 +226,15 @@ def tile_denseattentiononehead_pa_kernel(tc, hidden_states, W_q, cos, sin, out):
                 wq(0)
             if i == 2:
                 wq(1)
+            if i >= 2:
+                add_p(i - 1, 1, 1, nc.vector)
             if i >= 1:
                 quant(i - 1)
             if i == 0:
                 add_b(0, 1, nc.gpsimd)
             else:
                 add_g(i, 0, nc.gpsimd)
-                add_g(i, 1, nc.vector if i == 6 else nc.gpsimd)
+                add_p(i, 0, 1, nc.gpsimd)
             if i == 2:
                 mx(0, 0)
                 mx(0, 1)
@@ -234,6 +242,7 @@ def tile_denseattentiononehead_pa_kernel(tc, hidden_states, W_q, cos, sin, out):
                 mx(i - 1, 0)
                 mx(i - 1, 1)
         mul(7, 0)
+        add_p(6, 1, 1, nc.vector)
         quant(6)
         add_b(7, 0, nc.gpsimd)
         mx(6, 0)

@@ -12,12 +12,12 @@ U8 = mybir.dt.uint8
 FP8X4 = mybir.dt.float8_e4m3fn_x4
 MULT = mybir.AluOpType.mult
 ADD = mybir.AluOpType.add
-SUB = mybir.AluOpType.subtract
 
 P = 128
 B = 2
 H = 1024
 NT = 8
+NWARM = 5
 CHUNKS = [(0, 1), (1, 2), (2, 3), (3, 4), (4, 6), (6, 8)]
 
 
@@ -72,6 +72,12 @@ def tile_denseattentiononehead_pa_kernel(tc, hidden_states, W_q, cos, sin, out):
         load(4)
         load(5)
 
+        warm = res.tile([P, 512], BF16, name="warm")
+        nc.vector.memset(warm[:], 0.0)
+        wacc = pa.tile([P, 512], F32, name="wacc", tag="acc")
+        for k in range(NWARM):
+            nc.tensor.matmul(out=wacc[:], lhsT=warm[:, 0:P], rhs=warm[:], start=True, stop=True)
+
         def word_t(dst, src, swap):
             for u in range(2):
                 for g in range(2):
@@ -101,7 +107,13 @@ def tile_denseattentiononehead_pa_kernel(tc, hidden_states, W_q, cos, sin, out):
             sb = tp.tile([P, 512], F32, name="sb", tag="tp")
             word_t(sb, sin_sb[:, i, :].bitcast(F32), True)
             sin_t = tabs.tile([P, H], BF16, name="sin_t", tag="sin_t")
-            pairs_out(sin_t[:], sb)
+            nc.scalar.copy(
+                out=sin_t[:, 0:512].bitcast(F32).rearrange("p (r u) -> p r u", u=2),
+                in_=sb[:].rearrange("p (u g r) -> p g r u", u=2, g=2)[:, 0, :, :])
+            nc.scalar.mul(
+                out=sin_t[:, 512:1024].rearrange("p (r u e) -> p r u e", u=2, e=2),
+                in_=sb[:].bitcast(BF16).rearrange("p (u g r e) -> p g r u e", u=2, g=2, e=2)[:, 1, :, :, :],
+                mul=-1.0)
             tab[(i, 1)] = sin_t
 
         def x_t(i, b):
@@ -114,15 +126,15 @@ def tile_denseattentiononehead_pa_kernel(tc, hidden_states, W_q, cos, sin, out):
 
         def mul(i, b):
             if b == 0:
-                t1n = prod.tile([P, B, H], F32, name="t1", tag="t1")
-                t2n = prod.tile([P, B, H], F32, name="t2", tag="t2")
+                t1n = prod.tile([P, B, 2, 512], F32, name="t1", tag="t1")
+                t2n = prod.tile([P, B, 2, 512], F32, name="t2", tag="t2")
                 tiles[i] = (t1n, t2n)
             t1, t2 = tiles[i]
             cos_t = tab[(i, 0)]
             sin_t = tab[(i, 1)]
             xin = xbs[(i, b)][:].bitcast(BF16).rearrange("p (u r e) -> p r u e", u=2, e=2)
-            nc.vector.tensor_tensor(out=rue(t1[:, b, :]), in0=xin, in1=rue(cos_t[:]), op=MULT)
-            nc.vector.tensor_tensor(out=rue(t2[:, b, :]), in0=xin, in1=rue(sin_t[:]), op=MULT)
+            nc.vector.tensor_tensor(out=rue(t1[:, b, :, :].rearrange("p g c -> p (g c)")), in0=xin, in1=rue(cos_t[:]), op=MULT)
+            nc.vector.tensor_tensor(out=rue(t2[:, b, :, :].rearrange("p g c -> p (g c)")), in0=xin, in1=rue(sin_t[:]), op=MULT)
 
         def grp_of(i):
             if i not in grps:
@@ -130,24 +142,15 @@ def tile_denseattentiononehead_pa_kernel(tc, hidden_states, W_q, cos, sin, out):
                 grps[i] = grpn
             return grps[i]
 
-        def add_g(i, g, eng):
+        def add_all(i, eng):
             grp = grp_of(i)
             t1, t2 = tiles[i]
-            eng.tensor_tensor(out=grp[:, :, g, :], in0=t1[:, :, 512 * g:512 * g + 512],
-                              in1=t2[:, :, 512 * (1 - g):512 * (1 - g) + 512], op=(SUB if g == 0 else ADD))
-
-        def add_p(i, b, g, eng):
-            grp = grp_of(i)
-            t1, t2 = tiles[i]
-            eng.tensor_tensor(out=grp[:, b, g, :], in0=t1[:, b, 512 * g:512 * g + 512],
-                              in1=t2[:, b, 512 * (1 - g):512 * (1 - g) + 512], op=(SUB if g == 0 else ADD))
+            eng.tensor_tensor(out=grp[:], in0=t1[:], in1=t2[:, :, ::-1, :], op=ADD)
 
         def add_b(i, b, eng):
             grp = grp_of(i)
             t1, t2 = tiles[i]
-            for g in range(2):
-                eng.tensor_tensor(out=grp[:, b, g, :], in0=t1[:, b, 512 * g:512 * g + 512],
-                                  in1=t2[:, b, 512 * (1 - g):512 * (1 - g) + 512], op=(SUB if g == 0 else ADD))
+            eng.tensor_tensor(out=grp[:, b, :, :], in0=t1[:, b, :, :], in1=t2[:, b, ::-1, :], op=ADD)
 
         def quant_b(i, b):
             nc.vector.quantize_mx(
@@ -226,15 +229,16 @@ def tile_denseattentiononehead_pa_kernel(tc, hidden_states, W_q, cos, sin, out):
                 wq(0)
             if i == 2:
                 wq(1)
-            if i >= 2:
-                add_p(i - 1, 1, 1, nc.vector)
             if i >= 1:
                 quant(i - 1)
             if i == 0:
                 add_b(0, 1, nc.gpsimd)
             else:
-                add_g(i, 0, nc.gpsimd)
-                add_p(i, 0, 1, nc.gpsimd)
+                if i == 6:
+                    add_b(6, 0, nc.gpsimd)
+                    add_b(6, 1, nc.vector)
+                else:
+                    add_all(i, nc.gpsimd)
             if i == 2:
                 mx(0, 0)
                 mx(0, 1)
@@ -242,7 +246,6 @@ def tile_denseattentiononehead_pa_kernel(tc, hidden_states, W_q, cos, sin, out):
                 mx(i - 1, 0)
                 mx(i - 1, 1)
         mul(7, 0)
-        add_p(6, 1, 1, nc.vector)
         quant(6)
         add_b(7, 0, nc.gpsimd)
         mx(6, 0)

@@ -18,7 +18,6 @@ B = 2
 H = 1024
 NT = 8
 NWARM = 5
-CHUNKS = [(0, 1), (1, 2), (2, 3), (3, 4), (4, 6), (6, 8)]
 
 
 def tile_denseattentiononehead_pa_kernel(tc, hidden_states, W_q, cos, sin, out):
@@ -33,10 +32,11 @@ def tile_denseattentiononehead_pa_kernel(tc, hidden_states, W_q, cos, sin, out):
         prod = ctx.enter_context(tc.tile_pool(name="prod", bufs=3))
         tabs = ctx.enter_context(tc.tile_pool(name="tabs", bufs=2))
         gpool = ctx.enter_context(tc.tile_pool(name="gpool", bufs=1))
-        opool = ctx.enter_context(tc.tile_pool(name="opool", bufs=3))
-        px = ctx.enter_context(tc.psum_pool(name="px", bufs=4))
-        tp = ctx.enter_context(tc.psum_pool(name="tp", bufs=2))
-        pa = ctx.enter_context(tc.psum_pool(name="pa", bufs=2))
+        dpool = ctx.enter_context(tc.tile_pool(name="dpool", bufs=2))
+        opool = ctx.enter_context(tc.tile_pool(name="opool", bufs=5))
+        px = ctx.enter_context(tc.psum_pool(name="px", bufs=2))
+        tp = ctx.enter_context(tc.psum_pool(name="tp", bufs=3))
+        pa = ctx.enter_context(tc.psum_pool(name="pa", bufs=3))
         ctx.enter_context(tc.manual_schedule())
 
         x0_sb = res.tile([P, NT, H], BF16, name="x0_sb")
@@ -50,28 +50,68 @@ def tile_denseattentiononehead_pa_kernel(tc, hidden_states, W_q, cos, sin, out):
         ws = res.tile([P, 2, H], U8, name="ws", align_bytes=64)
         hc = res.tile([P, NT, 512], U32, name="hc", align_bytes=64)
         hs = res.tile([P, NT, 512], U8, name="hs", align_bytes=64)
+        t1z = res.tile([P, B, 2, 512], F32, name="t1z")
+        t2z = res.tile([P, B, 2, 512], F32, name="t2z")
         ident = res.tile([P, P], F32, name="ident")
+        identb = res.tile([P, P], BF16, name="identb")
 
-        def load(c):
-            t0, t1 = CHUNKS[c]
+        def load_cos(t0, t1=None):
+            t1 = t1 or t0 + 1
             nc.sync.dma_start(out=cos_sb[:, t0:t1, :], in_=cv[:, t0:t1, :])
-            nc.sync.dma_start(out=x_sb[0][:, t0:t1, :], in_=xv[:, 0, t0:t1, :])
+
+        def load_sin(t0, t1=None):
+            t1 = t1 or t0 + 1
             nc.sync.dma_start(out=sin_sb[:, t0:t1, :], in_=sv[:, t0:t1, :])
-            nc.sync.dma_start(out=x_sb[1][:, t0:t1, :], in_=xv[:, 1, t0:t1, :])
+
+        def load_x(b, t0, t1=None):
+            t1 = t1 or t0 + 1
+            nc.sync.dma_start(out=x_sb[b][:, t0:t1, :], in_=xv[:, b, t0:t1, :])
+
+        def load(t0, t1):
+            load_cos(t0, t1)
+            load_x(0, t0, t1)
+            load_sin(t0, t1)
+            load_x(1, t0, t1)
 
         def load_w(a):
             nc.sync.dma_start(out=w_sb[:, 4 * a:4 * a + 4, :], in_=wv[:, 4 * a:4 * a + 4, :])
 
+        make_identity(nc, identb[:])
         make_identity(nc, ident[:])
-        load(0)
-        load(1)
+        load_x(0, 1)
+        load_cos(1)
+        load_x(0, 0)
+        load_sin(1)
+        load_cos(0)
+        load_x(1, 1)
+        load_sin(0)
+        load_x(1, 0)
+        load_cos(2)
+        load_x(0, 2)
+        load_sin(2)
+        load_x(1, 2)
         load_w(0)
-        load(2)
+        load_cos(3)
+        load_x(0, 3)
+        load_sin(3)
+        load_x(1, 3)
         load_w(1)
-        load(3)
-        load(4)
-        load(5)
-
+        load_cos(4)
+        load_x(0, 4)
+        load_sin(4)
+        load_x(1, 4)
+        load_cos(5)
+        load_x(0, 5)
+        load_sin(5)
+        load_x(1, 5)
+        load_cos(6)
+        load_x(0, 6)
+        load_sin(6)
+        load_x(1, 6)
+        load_cos(7)
+        load_x(0, 7)
+        load_sin(7)
+        load_x(1, 7)
         warm = res.tile([P, 512], BF16, name="warm")
         nc.vector.memset(warm[:], 0.0)
         wacc = pa.tile([P, 512], F32, name="wacc", tag="acc")
@@ -92,9 +132,11 @@ def tile_denseattentiononehead_pa_kernel(tc, hidden_states, W_q, cos, sin, out):
 
         tab = {}
         xbs = {}
-        tiles = {}
+        tiles = {0: (t1z, t2z)}
         grps = {}
         outs = {}
+        negs = {}
+
 
         def cos_tr(i):
             cb = tp.tile([P, 512], F32, name="cb", tag="tp")
@@ -124,17 +166,16 @@ def tile_denseattentiononehead_pa_kernel(tc, hidden_states, W_q, cos, sin, out):
         def rue(ap):
             return ap.rearrange("p (r u e) -> p r u e", u=2, e=2)
 
-        def mul(i, b):
-            if b == 0:
-                t1n = prod.tile([P, B, 2, 512], F32, name="t1", tag="t1")
-                t2n = prod.tile([P, B, 2, 512], F32, name="t2", tag="t2")
-                tiles[i] = (t1n, t2n)
-            t1, t2 = tiles[i]
-            cos_t = tab[(i, 0)]
-            sin_t = tab[(i, 1)]
+        def new_prod(i):
+            t1n = prod.tile([P, B, 2, 512], F32, name="t1", tag="t1")
+            t2n = prod.tile([P, B, 2, 512], F32, name="t2", tag="t2")
+            tiles[i] = (t1n, t2n)
+
+        def a_mul(i, b, k):
+            if i not in tiles:
+                new_prod(i)
             xin = xbs[(i, b)][:].bitcast(BF16).rearrange("p (u r e) -> p r u e", u=2, e=2)
-            nc.vector.tensor_tensor(out=rue(t1[:, b, :, :].rearrange("p g c -> p (g c)")), in0=xin, in1=rue(cos_t[:]), op=MULT)
-            nc.vector.tensor_tensor(out=rue(t2[:, b, :, :].rearrange("p g c -> p (g c)")), in0=xin, in1=rue(sin_t[:]), op=MULT)
+            nc.vector.tensor_tensor(out=rue(tiles[i][k][:, b, :, :].rearrange("p g c -> p (g c)")), in0=xin, in1=rue(tab[(i, k)][:]), op=MULT)
 
         def grp_of(i):
             if i not in grps:
@@ -152,6 +193,72 @@ def tile_denseattentiononehead_pa_kernel(tc, hidden_states, W_q, cos, sin, out):
             t1, t2 = tiles[i]
             eng.tensor_tensor(out=grp[:, b, :, :], in0=t1[:, b, :, :], in1=t2[:, b, ::-1, :], op=ADD)
 
+        def t_all(i):
+            cos_tr(i)
+            x_t(i, 0)
+            sin_tr(i)
+            x_t(i, 1)
+
+
+        def neg(i):
+            sneg = dpool.tile([P, 512], BF16, name="sneg", tag="sneg")
+            nc.scalar.mul(out=sneg[:], in_=sin_sb[:, i, 0:512], mul=-1.0)
+            negs[i] = sneg
+
+        def d_x(i, b):
+            xn = px.tile([P, H], BF16, name="xn", tag="xb")
+            for h in range(2):
+                c = slice(512 * h, 512 * h + 512)
+                nc.tensor.matmul(out=xn[:, c], lhsT=identb[:], rhs=x_sb[b][:, i, c], start=True, stop=True)
+            xbs[(i, b)] = xn
+
+        def weq(ap, w):
+            return ap.rearrange("p (w q e) -> p w e q", w=w, e=2)
+
+        def weq_out(ap, w):
+            return ap.rearrange("p (w e q) -> p w e q", w=w, e=2)
+
+        def n_mul(i, b, k, eng, x):
+            if i not in tiles:
+                new_prod(i)
+            t1, t2 = tiles[i]
+            if k == 0:
+                eng.tensor_tensor(out=weq_out(t1[:, b, :, :].rearrange("p g c -> p (g c)"), 4),
+                                  in0=weq(x, 4), in1=weq(cos_sb[:, i, :], 4), op=MULT)
+            elif k == 1:
+                eng.tensor_tensor(out=weq_out(t2[:, b, 1, :], 2),
+                                  in0=weq(x[:, 0:512], 2), in1=weq(sin_sb[:, i, 512:1024], 2), op=MULT)
+            else:
+                eng.tensor_tensor(out=weq_out(t2[:, b, 0, :], 2),
+                                  in0=weq(x[:, 512:1024], 2), in1=weq(negs[i][:], 2), op=MULT)
+
+        def c_mul(i, b, k):
+            n_mul(i, b, k, nc.gpsimd, x_sb[b][:, i, :])
+
+        def d_mul(i, b, k):
+            n_mul(i, b, k, nc.vector, xbs[(i, b)][:])
+
+        def s_mul(i, b, k):
+            n_mul(i, b, k, nc.vector, x_sb[b][:, i, :])
+
+        def p_add(i, b, g, v=False):
+            if i not in grps:
+                grpd = dpool.tile([P, B, 2, 512], BF16, name="grpd", tag="grpd", align_bytes=64)
+                grps[i] = grpd
+            t1, t2 = tiles[i]
+            hb = tp.tile([P, 512], F32, name="hb", tag="tp")
+            for t in range(4):
+                c = slice(t * P, (t + 1) * P)
+                nc.tensor.matmul(out=hb[:, c], lhsT=t1[:, b, g, c], rhs=ident[:], is_transpose=True, start=True, stop=False)
+                nc.tensor.matmul(out=hb[:, c], lhsT=t2[:, b, g, c], rhs=ident[:], is_transpose=True, start=False, stop=True)
+            h_out = grps[i][:, b, g, :].rearrange("p (r t) -> p r t", t=4)
+            h_in = hb[:].rearrange("p (t r) -> p r t", t=4)
+            if v:
+                nc.vector.tensor_copy(out=h_out, in_=h_in)
+            else:
+                nc.scalar.copy(out=h_out, in_=h_in)
+
+
         def quant_b(i, b):
             nc.vector.quantize_mx(
                 out=hc[:, i, 256 * b:256 * b + 256].bitcast(FP8X4),
@@ -163,96 +270,198 @@ def tile_denseattentiononehead_pa_kernel(tc, hidden_states, W_q, cos, sin, out):
                 out=hc[:, i, :].bitcast(FP8X4), scales=hs[:, i, :],
                 in_=grps[i][:].rearrange("p b g c -> p (b g c)"))
 
-        def wtr(a):
+        def wtr(a, g, h):
+            wb = tp.tile([P, 512], F32, name="wb", tag="tp")
+            for u in range(2):
+                for oi in range(2):
+                    src = w_sb[:, 4 * a + 2 * h + oi, :].bitcast(F32)
+                    nc.tensor.transpose(
+                        wb[:, u * 256 + oi * P:u * 256 + (oi + 1) * P],
+                        src[:, (2 * g + u) * P:(2 * g + u + 1) * P], ident[:])
+            o0 = (512 * a + 256 * h) * 4
+            pairs_out(wg[:, g, o0:o0 + 1024], wb)
+
+        def wq(a, g):
+            nc.vector.quantize_mx(
+                out=wc[:, g, 512 * a:512 * a + 512].bitcast(FP8X4),
+                scales=ws[:, g, 512 * a:512 * a + 512],
+                in_=wg[:, g, 2048 * a:2048 * a + 2048])
+
+        def mx(i, b, nh, v=False):
+            if (i, b) not in outs:
+                o_new = opool.tile([P, H], F32, name="o_sb", tag="o_sb")
+                outs[(i, b)] = o_new
+            o_sb = outs[(i, b)]
+            acc = pa.tile([P, 512], F32, name="acc", tag="acc")
             for g in range(2):
-                for h in range(2):
-                    wb = tp.tile([P, 512], F32, name="wb", tag="tp")
-                    for u in range(2):
-                        for oi in range(2):
-                            src = w_sb[:, 4 * a + 2 * h + oi, :].bitcast(F32)
-                            nc.tensor.transpose(
-                                wb[:, u * 256 + oi * P:u * 256 + (oi + 1) * P],
-                                src[:, (2 * g + u) * P:(2 * g + u + 1) * P], ident[:])
-                    o0 = (512 * a + 256 * h) * 4
-                    pairs_out(wg[:, g, o0:o0 + 1024], wb)
-
-        def wq(a):
-            for g in range(2):
-                nc.vector.quantize_mx(
-                    out=wc[:, g, 512 * a:512 * a + 512].bitcast(FP8X4),
-                    scales=ws[:, g, 512 * a:512 * a + 512],
-                    in_=wg[:, g, 2048 * a:2048 * a + 2048])
-
-        def mx(i, b, last=False, both=False):
-            if b == 0:
-                o_new = opool.tile([P, B, H], F32, name="o_sb", tag="o_sb")
-                outs[i] = o_new
-            o_sb = outs[i]
-            for nh in range(2):
-                acc = pa.tile([P, 512], F32, name="acc", tag="acc")
-                for g in range(2):
-                    m0 = (2 * b + g) * P
-                    nc.tensor.matmul_mx(
-                        out=acc[:],
-                        lhsT=hc[:, i, m0:m0 + P].bitcast(FP8X4),
-                        lhsT_scale=hs[:, i, m0:m0 + P],
-                        rhs=wc[:, g, 512 * nh:512 * nh + 512].bitcast(FP8X4),
-                        rhs_scale=ws[:, g, 512 * nh:512 * nh + 512],
-                        start=(g == 0), stop=(g == 1))
-                if both and nh == 1:
-                    nc.vector.tensor_copy(out=o_sb[:, b, 512 * nh:512 * nh + 512], in_=acc[:])
-                else:
-                    nc.scalar.copy(out=o_sb[:, b, 512 * nh:512 * nh + 512], in_=acc[:])
-            if last:
-                nc.sync.dma_start(out=ov[:, b, i, :], in_=o_sb[:, b, :])
-            elif b == 1:
-                nc.sync.dma_start(out=ov[:, :, i, :], in_=o_sb[:])
-
-        def t_all(i):
-            cos_tr(i)
-            x_t(i, 0)
-            sin_tr(i)
-            x_t(i, 1)
-
-        t_all(0)
-        t_all(1)
-        for i in range(7):
-            mul(i, 0)
-            if i == 0:
-                add_b(0, 0, nc.gpsimd)
-            mul(i, 1)
-            if i < 2:
-                wtr(i)
-            if i + 2 < NT:
-                t_all(i + 2)
-            if i == 1:
-                wq(0)
-            if i == 2:
-                wq(1)
-            if i >= 1:
-                quant(i - 1)
-            if i == 0:
-                add_b(0, 1, nc.gpsimd)
+                m0 = (2 * b + g) * P
+                nc.tensor.matmul_mx(
+                    out=acc[:],
+                    lhsT=hc[:, i, m0:m0 + P].bitcast(FP8X4),
+                    lhsT_scale=hs[:, i, m0:m0 + P],
+                    rhs=wc[:, g, 512 * nh:512 * nh + 512].bitcast(FP8X4),
+                    rhs_scale=ws[:, g, 512 * nh:512 * nh + 512],
+                    start=(g == 0), stop=(g == 1))
+            if v:
+                nc.vector.tensor_copy(out=o_sb[:, 512 * nh:512 * nh + 512], in_=acc[:])
             else:
-                if i == 6:
-                    add_b(6, 0, nc.gpsimd)
-                    add_b(6, 1, nc.vector)
-                else:
-                    add_all(i, nc.gpsimd)
-            if i == 2:
-                mx(0, 0)
-                mx(0, 1)
-            if i >= 2:
-                mx(i - 1, 0)
-                mx(i - 1, 1)
-        mul(7, 0)
-        quant(6)
+                nc.scalar.copy(out=o_sb[:, 512 * nh:512 * nh + 512], in_=acc[:])
+
+        def store(i, b, nh=None):
+            c = slice(0, H) if nh is None else slice(512 * nh, 512 * nh + 512)
+            nc.sync.dma_start(out=ov[:, b, i, c], in_=outs[(i, b)][:, c])
+
+        neg(1)
+        neg(0)
+        c_mul(0, 0, 0)
+        c_mul(0, 0, 1)
+        c_mul(0, 0, 2)
+        c_mul(0, 1, 0)
+        c_mul(0, 1, 1)
+        c_mul(0, 1, 2)
+        d_x(1, 0)
+        d_mul(1, 0, 0)
+        d_mul(1, 0, 1)
+        d_mul(1, 0, 2)
+        d_x(1, 1)
+        d_mul(1, 1, 0)
+        d_mul(1, 1, 1)
+        d_mul(1, 1, 2)
+        p_add(1, 0, 1)
+        cos_tr(2)
+        x_t(2, 0)
+        sin_tr(2)
+        p_add(1, 0, 0)
+        a_mul(2, 0, 0)
+        a_mul(2, 0, 1)
+        x_t(2, 1)
+        a_mul(2, 1, 0)
+        a_mul(2, 1, 1)
+        p_add(1, 1, 1)
+        cos_tr(3)
+        x_t(3, 0)
+        p_add(1, 1, 0)
+        sin_tr(3)
+        add_all(2, nc.gpsimd)
+        quant_b(1, 0)
+        wtr(0, 0, 0)
+        p_add(0, 0, 1)
+        wtr(0, 0, 1)
+        p_add(0, 0, 0)
+        x_t(3, 1)
+        a_mul(3, 0, 0)
+        a_mul(3, 0, 1)
+        a_mul(3, 1, 0)
+        a_mul(3, 1, 1)
+        wtr(0, 1, 0)
+        wtr(0, 1, 1)
+        p_add(0, 1, 1)
+        wtr(1, 0, 0)
+        p_add(0, 1, 0)
+        wtr(1, 0, 1)
+        wtr(1, 1, 0)
+        wtr(1, 1, 1)
+        x_t(4, 0)
+        cos_tr(4)
+        sin_tr(4)
+        x_t(4, 1)
+        quant_b(1, 1)
+        wq(0, 0)
+        wq(0, 1)
+        quant_b(0, 0)
+        quant_b(0, 1)
+        quant(2)
+        wq(1, 0)
+        wq(1, 1)
+        add_all(3, nc.gpsimd)
+        a_mul(4, 0, 0)
+        a_mul(4, 0, 1)
+        mx(1, 0, 0)
+        mx(1, 0, 1)
+        store(1, 0)
+        mx(1, 1, 0)
+        mx(1, 1, 1)
+        store(1, 1)
+        x_t(5, 0)
+        cos_tr(5)
+        mx(0, 0, 0)
+        mx(0, 0, 1)
+        store(0, 0)
+        a_mul(4, 1, 0)
+        a_mul(4, 1, 1)
+        sin_tr(5)
+        x_t(5, 1)
+        mx(0, 1, 0)
+        mx(0, 1, 1)
+        store(0, 1)
+        quant(3)
+        add_all(4, nc.gpsimd)
+        a_mul(5, 0, 0)
+        a_mul(5, 0, 1)
+        mx(2, 0, 0)
+        mx(2, 0, 1)
+        store(2, 0)
+        mx(2, 1, 0)
+        mx(2, 1, 1)
+        store(2, 1)
+        x_t(6, 0)
+        cos_tr(6)
+        mx(3, 0, 0)
+        mx(3, 0, 1)
+        store(3, 0)
+        a_mul(5, 1, 0)
+        a_mul(5, 1, 1)
+        sin_tr(6)
+        x_t(6, 1)
+        mx(3, 1, 0)
+        mx(3, 1, 1)
+        store(3, 1)
+        quant(4)
+        add_all(5, nc.gpsimd)
+        a_mul(6, 0, 0)
+        a_mul(6, 0, 1)
+        mx(4, 0, 0)
+        mx(4, 0, 1)
+        store(4, 0)
+        x_t(7, 0)
+        cos_tr(7)
+        a_mul(6, 1, 0)
+        a_mul(6, 1, 1)
+        sin_tr(7)
+        x_t(7, 1)
+        mx(4, 1, 0)
+        mx(4, 1, 1)
+        store(4, 1)
+        quant(5)
+        add_b(6, 0, nc.gpsimd)
+        a_mul(7, 0, 0)
+        a_mul(7, 0, 1)
+        mx(5, 0, 0)
+        mx(5, 0, 1)
+        store(5, 0)
+        mx(5, 1, 0)
+        mx(5, 1, 1)
+        store(5, 1)
+        quant_b(6, 0)
+        add_b(6, 1, nc.vector)
+        quant_b(6, 1)
         add_b(7, 0, nc.gpsimd)
-        mx(6, 0)
-        mx(6, 1)
-        mul(7, 1)
+        a_mul(7, 1, 0)
+        a_mul(7, 1, 1)
+        mx(6, 0, 0)
+        mx(6, 0, 1)
+        store(6, 0)
+        mx(6, 1, 0)
+        mx(6, 1, 1)
+        store(6, 1)
         quant_b(7, 0)
-        mx(7, 0, True)
         add_b(7, 1, nc.vector)
         quant_b(7, 1)
-        mx(7, 1, True, True)
+        mx(7, 0, 0)
+        store(7, 0, 0)
+        mx(7, 0, 1)
+        store(7, 0, 1)
+        mx(7, 1, 0)
+        store(7, 1, 0)
+        mx(7, 1, 1, True)
+        store(7, 1, 1)

@@ -78,24 +78,24 @@ def tile_denseattentiononehead_pa_kernel(tc, hidden_states, W_q, cos, sin, out):
 
         make_identity(nc, identb[:])
         make_identity(nc, ident[:])
-        load_x(0, 1)
-        load_cos(1)
         load_x(0, 0)
-        load_sin(1)
         load_cos(0)
-        load_x(1, 1)
         load_sin(0)
         load_x(1, 0)
+        load_cos(1)
+        load_x(0, 1)
+        load_sin(1)
+        load_x(1, 1)
+        load_w(0)
         load_cos(2)
         load_x(0, 2)
         load_sin(2)
         load_x(1, 2)
-        load_w(0)
+        load_w(1)
         load_cos(3)
         load_x(0, 3)
         load_sin(3)
         load_x(1, 3)
-        load_w(1)
         load_cos(4)
         load_x(0, 4)
         load_sin(4)
@@ -311,155 +311,153 @@ def tile_denseattentiononehead_pa_kernel(tc, hidden_states, W_q, cos, sin, out):
             c = slice(0, H) if nh is None else slice(512 * nh, 512 * nh + 512)
             nc.sync.dma_start(out=ov[:, b, i, c], in_=outs[(i, b)][:, c])
 
-        neg(1)
         neg(0)
-        c_mul(0, 0, 0)
-        c_mul(0, 0, 1)
-        c_mul(0, 0, 2)
-        c_mul(0, 1, 0)
-        c_mul(0, 1, 1)
-        c_mul(0, 1, 2)
-        d_x(1, 0)
-        d_mul(1, 0, 0)
-        d_mul(1, 0, 1)
-        d_mul(1, 0, 2)
-        d_x(1, 1)
-        d_mul(1, 1, 0)
-        d_mul(1, 1, 1)
-        d_mul(1, 1, 2)
-        p_add(1, 0, 1)
-        cos_tr(2)
+        s_mul(0, 0, 0)
+        s_mul(0, 0, 1)
+        s_mul(0, 0, 2)
+        s_mul(0, 1, 0)
+        s_mul(0, 1, 1)
+        s_mul(0, 1, 2)
+        cos_tr(1)
+        x_t(1, 0)
+        sin_tr(1)
+        x_t(1, 1)
+        p_add(0, 0, 1)
+        wtr(0, 0, 0)
+        p_add(0, 0, 0)
+        wtr(0, 0, 1)
+        a_mul(1, 0, 0)
+        a_mul(1, 0, 1)
         x_t(2, 0)
+        cos_tr(2)
         sin_tr(2)
-        p_add(1, 0, 0)
+        p_add(0, 1, 1)
+        wtr(0, 1, 0)
+        p_add(0, 1, 0)
+        wtr(0, 1, 1)
+        a_mul(1, 1, 0)
+        a_mul(1, 1, 1)
+        x_t(2, 1)
+        add_all(1, nc.gpsimd)
+        wtr(1, 0, 0)
+        wtr(1, 0, 1)
         a_mul(2, 0, 0)
         a_mul(2, 0, 1)
-        x_t(2, 1)
-        a_mul(2, 1, 0)
-        a_mul(2, 1, 1)
-        p_add(1, 1, 1)
         cos_tr(3)
-        x_t(3, 0)
-        p_add(1, 1, 0)
-        sin_tr(3)
-        add_all(2, nc.gpsimd)
-        quant_b(1, 0)
-        wtr(0, 0, 0)
-        p_add(0, 0, 1)
-        wtr(0, 0, 1)
-        p_add(0, 0, 0)
-        x_t(3, 1)
-        a_mul(3, 0, 0)
-        a_mul(3, 0, 1)
-        a_mul(3, 1, 0)
-        a_mul(3, 1, 1)
-        wtr(0, 1, 0)
-        wtr(0, 1, 1)
-        p_add(0, 1, 1)
-        wtr(1, 0, 0)
-        p_add(0, 1, 0)
-        wtr(1, 0, 1)
         wtr(1, 1, 0)
         wtr(1, 1, 1)
-        x_t(4, 0)
-        cos_tr(4)
-        sin_tr(4)
-        x_t(4, 1)
-        quant_b(1, 1)
-        wq(0, 0)
-        wq(0, 1)
+        sin_tr(3)
+        x_t(3, 0)
+        a_mul(2, 1, 0)
+        a_mul(2, 1, 1)
+        x_t(3, 1)
         quant_b(0, 0)
         quant_b(0, 1)
-        quant(2)
+        wq(0, 0)
+        wq(0, 1)
         wq(1, 0)
         wq(1, 1)
-        add_all(3, nc.gpsimd)
-        a_mul(4, 0, 0)
-        a_mul(4, 0, 1)
-        mx(1, 0, 0)
-        mx(1, 0, 1)
-        store(1, 0)
-        mx(1, 1, 0)
-        mx(1, 1, 1)
-        store(1, 1)
-        x_t(5, 0)
-        cos_tr(5)
+        quant(1)
+        add_all(2, nc.gpsimd)
+        a_mul(3, 0, 0)
+        a_mul(3, 0, 1)
         mx(0, 0, 0)
         mx(0, 0, 1)
         store(0, 0)
-        a_mul(4, 1, 0)
-        a_mul(4, 1, 1)
-        sin_tr(5)
-        x_t(5, 1)
         mx(0, 1, 0)
         mx(0, 1, 1)
         store(0, 1)
+        mx(1, 0, 0)
+        mx(1, 0, 1)
+        store(1, 0)
+        x_t(4, 0)
+        cos_tr(4)
+        sin_tr(4)
+        a_mul(3, 1, 0)
+        a_mul(3, 1, 1)
+        x_t(4, 1)
+        mx(1, 1, 0)
+        mx(1, 1, 1)
+        store(1, 1)
+        quant(2)
+        add_all(3, nc.gpsimd)
+        a_mul(4, 0, 0)
+        a_mul(4, 0, 1)
+        mx(2, 0, 0)
+        mx(2, 0, 1)
+        store(2, 0)
+        x_t(5, 0)
+        cos_tr(5)
+        sin_tr(5)
+        a_mul(4, 1, 0)
+        a_mul(4, 1, 1)
+        x_t(5, 1)
+        mx(2, 1, 0)
+        mx(2, 1, 1)
+        store(2, 1)
         quant(3)
         add_all(4, nc.gpsimd)
         a_mul(5, 0, 0)
         a_mul(5, 0, 1)
-        mx(2, 0, 0)
-        mx(2, 0, 1)
-        store(2, 0)
-        mx(2, 1, 0)
-        mx(2, 1, 1)
-        store(2, 1)
-        x_t(6, 0)
-        cos_tr(6)
         mx(3, 0, 0)
         mx(3, 0, 1)
         store(3, 0)
+        neg(6)
+        d_x(6, 0)
         a_mul(5, 1, 0)
         a_mul(5, 1, 1)
-        sin_tr(6)
-        x_t(6, 1)
+        d_x(6, 1)
         mx(3, 1, 0)
         mx(3, 1, 1)
         store(3, 1)
         quant(4)
         add_all(5, nc.gpsimd)
-        a_mul(6, 0, 0)
-        a_mul(6, 0, 1)
+        d_mul(6, 0, 0)
+        d_mul(6, 0, 1)
+        d_mul(6, 0, 2)
         mx(4, 0, 0)
         mx(4, 0, 1)
         store(4, 0)
         x_t(7, 0)
         cos_tr(7)
-        a_mul(6, 1, 0)
-        a_mul(6, 1, 1)
         sin_tr(7)
+        p_add(6, 0, 1)
+        p_add(6, 0, 0)
+        d_mul(6, 1, 0)
+        d_mul(6, 1, 1)
+        d_mul(6, 1, 2)
         x_t(7, 1)
         mx(4, 1, 0)
         mx(4, 1, 1)
         store(4, 1)
         quant(5)
-        add_b(6, 0, nc.gpsimd)
+        quant_b(6, 0)
         a_mul(7, 0, 0)
         a_mul(7, 0, 1)
-        mx(5, 0, 0)
-        mx(5, 0, 1)
-        store(5, 0)
-        mx(5, 1, 0)
-        mx(5, 1, 1)
-        store(5, 1)
-        quant_b(6, 0)
-        add_b(6, 1, nc.vector)
-        quant_b(6, 1)
         add_b(7, 0, nc.gpsimd)
         a_mul(7, 1, 0)
         a_mul(7, 1, 1)
+        mx(5, 0, 0)
+        mx(5, 0, 1)
+        store(5, 0)
+        p_add(6, 1, 1)
+        p_add(6, 1, 0)
+        mx(5, 1, 0)
+        mx(5, 1, 1)
+        store(5, 1)
+        quant_b(6, 1)
+        quant_b(7, 0)
+        add_b(7, 1, nc.vector)
+        quant_b(7, 1)
         mx(6, 0, 0)
         mx(6, 0, 1)
         store(6, 0)
         mx(6, 1, 0)
         mx(6, 1, 1)
         store(6, 1)
-        quant_b(7, 0)
-        add_b(7, 1, nc.vector)
-        quant_b(7, 1)
         mx(7, 0, 0)
         store(7, 0, 0)
-        mx(7, 0, 1)
+        mx(7, 0, 1, True)
         store(7, 0, 1)
         mx(7, 1, 0)
         store(7, 1, 0)

@@ -29,13 +29,13 @@ def tile_denseattentiononehead_pa_kernel(tc, hidden_states, W_q, cos, sin, out):
     ov = out.rearrange("b (q t) o -> q b t o", t=NT)
     with ExitStack() as ctx:
         res = ctx.enter_context(tc.tile_pool(name="res", bufs=1))
-        prod = ctx.enter_context(tc.tile_pool(name="prod", bufs=3))
+        prod = ctx.enter_context(tc.tile_pool(name="prod", bufs=4))
         tabs = ctx.enter_context(tc.tile_pool(name="tabs", bufs=2))
         gpool = ctx.enter_context(tc.tile_pool(name="gpool", bufs=1))
         dpool = ctx.enter_context(tc.tile_pool(name="dpool", bufs=2))
         opool = ctx.enter_context(tc.tile_pool(name="opool", bufs=5))
-        px = ctx.enter_context(tc.psum_pool(name="px", bufs=2))
-        tp = ctx.enter_context(tc.psum_pool(name="tp", bufs=3))
+        px = ctx.enter_context(tc.psum_pool(name="px", bufs=3))
+        tp = ctx.enter_context(tc.psum_pool(name="tp", bufs=2))
         pa = ctx.enter_context(tc.psum_pool(name="pa", bufs=3))
         ctx.enter_context(tc.manual_schedule())
 
@@ -50,8 +50,6 @@ def tile_denseattentiononehead_pa_kernel(tc, hidden_states, W_q, cos, sin, out):
         ws = res.tile([P, 2, H], U8, name="ws", align_bytes=64)
         hc = res.tile([P, NT, 512], U32, name="hc", align_bytes=64)
         hs = res.tile([P, NT, 512], U8, name="hs", align_bytes=64)
-        t1z = res.tile([P, B, 2, 512], F32, name="t1z")
-        t2z = res.tile([P, B, 2, 512], F32, name="t2z")
         ident = res.tile([P, P], F32, name="ident")
         identb = res.tile([P, P], BF16, name="identb")
 
@@ -86,16 +84,16 @@ def tile_denseattentiononehead_pa_kernel(tc, hidden_states, W_q, cos, sin, out):
         load_x(0, 1)
         load_sin(1)
         load_x(1, 1)
-        load_w(0)
         load_cos(2)
         load_x(0, 2)
         load_sin(2)
         load_x(1, 2)
-        load_w(1)
+        load_w(0)
         load_cos(3)
         load_x(0, 3)
         load_sin(3)
         load_x(1, 3)
+        load_w(1)
         load_cos(4)
         load_x(0, 4)
         load_sin(4)
@@ -132,10 +130,9 @@ def tile_denseattentiononehead_pa_kernel(tc, hidden_states, W_q, cos, sin, out):
 
         tab = {}
         xbs = {}
-        tiles = {0: (t1z, t2z)}
+        tiles = {}
         grps = {}
         outs = {}
-        negs = {}
 
 
         def cos_tr(i):
@@ -200,11 +197,6 @@ def tile_denseattentiononehead_pa_kernel(tc, hidden_states, W_q, cos, sin, out):
             x_t(i, 1)
 
 
-        def neg(i):
-            sneg = dpool.tile([P, 512], BF16, name="sneg", tag="sneg")
-            nc.scalar.mul(out=sneg[:], in_=sin_sb[:, i, 0:512], mul=-1.0)
-            negs[i] = sneg
-
         def d_x(i, b):
             xn = px.tile([P, H], BF16, name="xn", tag="xb")
             for h in range(2):
@@ -229,11 +221,11 @@ def tile_denseattentiononehead_pa_kernel(tc, hidden_states, W_q, cos, sin, out):
                 eng.tensor_tensor(out=weq_out(t2[:, b, 1, :], 2),
                                   in0=weq(x[:, 0:512], 2), in1=weq(sin_sb[:, i, 512:1024], 2), op=MULT)
             else:
-                eng.tensor_tensor(out=weq_out(t2[:, b, 0, :], 2),
-                                  in0=weq(x[:, 512:1024], 2), in1=weq(negs[i][:], 2), op=MULT)
-
-        def c_mul(i, b, k):
-            n_mul(i, b, k, nc.gpsimd, x_sb[b][:, i, :])
+                for u in range(2):
+                    c = slice(256 * u, 256 * u + 256)
+                    eng.scalar_tensor_tensor(out=t2[:, b, 0, c].rearrange("p (e q) -> p e q", e=2),
+                                             in0=x[:, 512:1024][:, c].rearrange("p (q e) -> p e q", e=2), scalar=-1.0,
+                                             in1=sin_sb[:, i, c].rearrange("p (q e) -> p e q", e=2), op0=MULT, op1=MULT)
 
         def d_mul(i, b, k):
             n_mul(i, b, k, nc.vector, xbs[(i, b)][:])
@@ -311,7 +303,6 @@ def tile_denseattentiononehead_pa_kernel(tc, hidden_states, W_q, cos, sin, out):
             c = slice(0, H) if nh is None else slice(512 * nh, 512 * nh + 512)
             nc.sync.dma_start(out=ov[:, b, i, c], in_=outs[(i, b)][:, c])
 
-        neg(0)
         s_mul(0, 0, 0)
         s_mul(0, 0, 1)
         s_mul(0, 0, 2)
@@ -321,140 +312,139 @@ def tile_denseattentiononehead_pa_kernel(tc, hidden_states, W_q, cos, sin, out):
         cos_tr(1)
         x_t(1, 0)
         sin_tr(1)
-        x_t(1, 1)
         p_add(0, 0, 1)
-        wtr(0, 0, 0)
+        x_t(1, 1)
         p_add(0, 0, 0)
-        wtr(0, 0, 1)
         a_mul(1, 0, 0)
         a_mul(1, 0, 1)
-        x_t(2, 0)
-        cos_tr(2)
-        sin_tr(2)
-        p_add(0, 1, 1)
-        wtr(0, 1, 0)
-        p_add(0, 1, 0)
-        wtr(0, 1, 1)
         a_mul(1, 1, 0)
         a_mul(1, 1, 1)
+        cos_tr(2)
+        x_t(2, 0)
+        sin_tr(2)
+        p_add(0, 1, 1)
+        p_add(0, 1, 0)
         x_t(2, 1)
         add_all(1, nc.gpsimd)
-        wtr(1, 0, 0)
-        wtr(1, 0, 1)
         a_mul(2, 0, 0)
         a_mul(2, 0, 1)
-        cos_tr(3)
-        wtr(1, 1, 0)
-        wtr(1, 1, 1)
-        sin_tr(3)
-        x_t(3, 0)
         a_mul(2, 1, 0)
         a_mul(2, 1, 1)
+        wtr(0, 0, 0)
+        wtr(0, 0, 1)
+        wtr(0, 1, 0)
+        wtr(0, 1, 1)
+        cos_tr(3)
+        x_t(3, 0)
+        sin_tr(3)
         x_t(3, 1)
-        quant_b(0, 0)
-        quant_b(0, 1)
         wq(0, 0)
         wq(0, 1)
-        wq(1, 0)
-        wq(1, 1)
+        quant_b(0, 0)
+        quant_b(0, 1)
         quant(1)
         add_all(2, nc.gpsimd)
         a_mul(3, 0, 0)
         a_mul(3, 0, 1)
-        mx(0, 0, 0)
-        mx(0, 0, 1)
-        store(0, 0)
-        mx(0, 1, 0)
-        mx(0, 1, 1)
-        store(0, 1)
-        mx(1, 0, 0)
-        mx(1, 0, 1)
-        store(1, 0)
-        x_t(4, 0)
-        cos_tr(4)
-        sin_tr(4)
         a_mul(3, 1, 0)
         a_mul(3, 1, 1)
-        x_t(4, 1)
+        wtr(1, 0, 0)
+        mx(1, 0, 0)
+        wtr(1, 0, 1)
         mx(1, 1, 0)
-        mx(1, 1, 1)
-        store(1, 1)
+        wtr(1, 1, 0)
+        mx(0, 0, 0)
+        wtr(1, 1, 1)
+        mx(0, 1, 0)
+        cos_tr(4)
+        x_t(4, 0)
+        sin_tr(4)
+        x_t(4, 1)
+        wq(1, 0)
+        wq(1, 1)
         quant(2)
         add_all(3, nc.gpsimd)
         a_mul(4, 0, 0)
         a_mul(4, 0, 1)
+        mx(1, 0, 1)
+        store(1, 0)
+        mx(1, 1, 1)
+        store(1, 1)
+        d_x(6, 1)
+        a_mul(4, 1, 0)
+        a_mul(4, 1, 1)
+        d_mul(6, 1, 1)
+        mx(0, 0, 1)
+        store(0, 0)
+        mx(0, 1, 1)
+        store(0, 1)
+        cos_tr(5)
+        x_t(5, 0)
+        sin_tr(5)
+        quant(3)
+        add_all(4, nc.gpsimd)
+        d_mul(6, 1, 0)
+        d_mul(6, 1, 2)
+        a_mul(5, 0, 0)
+        a_mul(5, 0, 1)
         mx(2, 0, 0)
         mx(2, 0, 1)
         store(2, 0)
-        x_t(5, 0)
-        cos_tr(5)
-        sin_tr(5)
-        a_mul(4, 1, 0)
-        a_mul(4, 1, 1)
         x_t(5, 1)
         mx(2, 1, 0)
         mx(2, 1, 1)
         store(2, 1)
-        quant(3)
-        add_all(4, nc.gpsimd)
-        a_mul(5, 0, 0)
-        a_mul(5, 0, 1)
+        p_add(6, 1, 1)
+        p_add(6, 1, 0)
+        a_mul(5, 1, 0)
+        a_mul(5, 1, 1)
+        quant(4)
+        add_all(5, nc.gpsimd)
+        quant_b(6, 1)
         mx(3, 0, 0)
         mx(3, 0, 1)
         store(3, 0)
-        neg(6)
         d_x(6, 0)
-        a_mul(5, 1, 0)
-        a_mul(5, 1, 1)
-        d_x(6, 1)
+        cos_tr(7)
         mx(3, 1, 0)
         mx(3, 1, 1)
         store(3, 1)
-        quant(4)
-        add_all(5, nc.gpsimd)
+        sin_tr(7)
         d_mul(6, 0, 0)
         d_mul(6, 0, 1)
         d_mul(6, 0, 2)
+        x_t(7, 0)
+        a_mul(7, 0, 0)
+        a_mul(7, 0, 1)
         mx(4, 0, 0)
         mx(4, 0, 1)
         store(4, 0)
-        x_t(7, 0)
-        cos_tr(7)
-        sin_tr(7)
+        mx(6, 1, 0)
+        mx(6, 1, 1)
+        store(6, 1)
         p_add(6, 0, 1)
         p_add(6, 0, 0)
-        d_mul(6, 1, 0)
-        d_mul(6, 1, 1)
-        d_mul(6, 1, 2)
-        x_t(7, 1)
         mx(4, 1, 0)
         mx(4, 1, 1)
         store(4, 1)
+        x_t(7, 1)
         quant(5)
         quant_b(6, 0)
-        a_mul(7, 0, 0)
-        a_mul(7, 0, 1)
         add_b(7, 0, nc.gpsimd)
         a_mul(7, 1, 0)
         a_mul(7, 1, 1)
         mx(5, 0, 0)
         mx(5, 0, 1)
         store(5, 0)
-        p_add(6, 1, 1)
-        p_add(6, 1, 0)
         mx(5, 1, 0)
         mx(5, 1, 1)
         store(5, 1)
-        quant_b(6, 1)
-        quant_b(7, 0)
-        add_b(7, 1, nc.vector)
-        quant_b(7, 1)
         mx(6, 0, 0)
         mx(6, 0, 1)
         store(6, 0)
-        mx(6, 1, 0)
-        mx(6, 1, 1)
-        store(6, 1)
+        quant_b(7, 0)
+        add_b(7, 1, nc.vector)
+        quant_b(7, 1)
         mx(7, 0, 0)
         store(7, 0, 0)
         mx(7, 0, 1, True)

@@ -65,6 +65,18 @@ def tile_denseattentiononehead_pa_kernel(tc, hidden_states, W_q, cos, sin, out):
             t1 = t1 or t0 + 1
             nc.sync.dma_start(out=x_sb[b][:, t0:t1, :], in_=xv[:, b, t0:t1, :])
 
+        def load_xh(b, i, g):
+            c = slice(512 * g, 512 * g + 512)
+            nc.sync.dma_start(out=x_sb[b][:, i, c], in_=xv[:, b, i, c])
+
+        def load_cosh(i, g):
+            c = slice(512 * g, 512 * g + 512)
+            nc.sync.dma_start(out=cos_sb[:, i, c], in_=cv[:, i, c])
+
+        def load_sinh(i, g):
+            c = slice(512 * g, 512 * g + 512)
+            nc.sync.dma_start(out=sin_sb[:, i, c], in_=sv[:, i, c])
+
         def load(t0, t1):
             load_cos(t0, t1)
             load_x(0, t0, t1)
@@ -76,9 +88,12 @@ def tile_denseattentiononehead_pa_kernel(tc, hidden_states, W_q, cos, sin, out):
 
         make_identity(nc, identb[:])
         make_identity(nc, ident[:])
-        load_x(0, 0)
-        load_cos(0)
-        load_sin(0)
+        load_xh(0, 0, 0)
+        load_cosh(0, 0)
+        load_sinh(0, 1)
+        load_xh(0, 0, 1)
+        load_cosh(0, 1)
+        load_sinh(0, 0)
         load_x(1, 0)
         load_cos(1)
         load_x(0, 1)
@@ -214,9 +229,9 @@ def tile_denseattentiononehead_pa_kernel(tc, hidden_states, W_q, cos, sin, out):
             if i not in tiles:
                 new_prod(i)
             t1, t2 = tiles[i]
-            if k == 0:
-                eng.tensor_tensor(out=weq_out(t1[:, b, :, :].rearrange("p g c -> p (g c)"), 4),
-                                  in0=weq(x, 4), in1=weq(cos_sb[:, i, :], 4), op=MULT)
+            if k in (0, 2):
+                c = slice(256 * k, 256 * k + 512)
+                eng.tensor_tensor(out=weq_out(t1[:, b, k // 2, :], 2), in0=weq(x[:, c], 2), in1=weq(cos_sb[:, i, c], 2), op=MULT)
             elif k == 1:
                 eng.tensor_tensor(out=weq_out(t2[:, b, 1, :], 2),
                                   in0=weq(x[:, 0:512], 2), in1=weq(sin_sb[:, i, 512:1024], 2), op=MULT)
@@ -248,7 +263,9 @@ def tile_denseattentiononehead_pa_kernel(tc, hidden_states, W_q, cos, sin, out):
             if v:
                 nc.vector.tensor_copy(out=h_out, in_=h_in)
             else:
-                nc.scalar.copy(out=h_out, in_=h_in)
+                nc.scalar.copy(
+                    out=grps[i][:, b, g, :].rearrange("p (c i t) -> p c t i", i=4, t=4),
+                    in_=hb[:].rearrange("p (t c i) -> p c t i", t=4, i=4))
 
 
         def quant_b(i, b):
@@ -306,9 +323,11 @@ def tile_denseattentiononehead_pa_kernel(tc, hidden_states, W_q, cos, sin, out):
         s_mul(0, 0, 0)
         s_mul(0, 0, 1)
         s_mul(0, 0, 2)
+        s_mul(0, 0, 3)
         s_mul(0, 1, 0)
         s_mul(0, 1, 1)
         s_mul(0, 1, 2)
+        s_mul(0, 1, 3)
         cos_tr(1)
         x_t(1, 0)
         sin_tr(1)
@@ -373,7 +392,7 @@ def tile_denseattentiononehead_pa_kernel(tc, hidden_states, W_q, cos, sin, out):
         d_x(6, 1)
         a_mul(4, 1, 0)
         a_mul(4, 1, 1)
-        d_mul(6, 1, 1)
+        d_mul(6, 1, 0)
         mx(0, 0, 1)
         store(0, 0)
         mx(0, 1, 1)
@@ -383,8 +402,9 @@ def tile_denseattentiononehead_pa_kernel(tc, hidden_states, W_q, cos, sin, out):
         sin_tr(5)
         quant(3)
         add_all(4, nc.gpsimd)
-        d_mul(6, 1, 0)
+        d_mul(6, 1, 1)
         d_mul(6, 1, 2)
+        d_mul(6, 1, 3)
         a_mul(5, 0, 0)
         a_mul(5, 0, 1)
         mx(2, 0, 0)
@@ -413,6 +433,7 @@ def tile_denseattentiononehead_pa_kernel(tc, hidden_states, W_q, cos, sin, out):
         d_mul(6, 0, 0)
         d_mul(6, 0, 1)
         d_mul(6, 0, 2)
+        d_mul(6, 0, 3)
         x_t(7, 0)
         a_mul(7, 0, 0)
         a_mul(7, 0, 1)

@@ -29,7 +29,7 @@ def tile_denseattentiononehead_pa_kernel(tc, hidden_states, W_q, cos, sin, out):
     ov = out.rearrange("b (q t) o -> q b t o", t=NT)
     with ExitStack() as ctx:
         res = ctx.enter_context(tc.tile_pool(name="res", bufs=1))
-        prod = ctx.enter_context(tc.tile_pool(name="prod", bufs=4))
+        prod = ctx.enter_context(tc.tile_pool(name="prod", bufs=3))
         tabs = ctx.enter_context(tc.tile_pool(name="tabs", bufs=2))
         gpool = ctx.enter_context(tc.tile_pool(name="gpool", bufs=1))
         dpool = ctx.enter_context(tc.tile_pool(name="dpool", bufs=2))
@@ -45,11 +45,13 @@ def tile_denseattentiononehead_pa_kernel(tc, hidden_states, W_q, cos, sin, out):
         cos_sb = res.tile([P, NT, H], BF16, name="cos_sb")
         sin_sb = res.tile([P, NT, H], BF16, name="sin_sb")
         w_sb = res.tile([P, NT, H], BF16, name="w_sb")
-        wg = res.tile([P, 2, 4 * H], BF16, name="wg", align_bytes=64)
-        wc = res.tile([P, 2, H], U32, name="wc", align_bytes=64)
-        ws = res.tile([P, 2, H], U8, name="ws", align_bytes=64)
+        wg = res.tile([P, 2, 2, 2048], BF16, name="wg", align_bytes=64)
+        wc = res.tile([P, 2, 2, 512], U32, name="wc", align_bytes=64)
+        ws = res.tile([P, 2, 2, 512], U8, name="ws", align_bytes=64)
         hc = res.tile([P, NT, 512], U32, name="hc", align_bytes=64)
         hs = res.tile([P, NT, 512], U8, name="hs", align_bytes=64)
+        t1d = res.tile([P, B, 2, 512], F32, name="t1d")
+        t2d = res.tile([P, B, 2, 512], F32, name="t2d")
         ident = res.tile([P, P], F32, name="ident")
         identb = res.tile([P, P], BF16, name="identb")
 
@@ -99,6 +101,8 @@ def tile_denseattentiononehead_pa_kernel(tc, hidden_states, W_q, cos, sin, out):
         load_x(0, 1)
         load_sin(1)
         load_x(1, 1)
+        load_cos(6)
+        load_x(1, 6)
         load_cos(2)
         load_x(0, 2)
         load_sin(2)
@@ -117,10 +121,8 @@ def tile_denseattentiononehead_pa_kernel(tc, hidden_states, W_q, cos, sin, out):
         load_x(0, 5)
         load_sin(5)
         load_x(1, 5)
-        load_cos(6)
         load_x(0, 6)
         load_sin(6)
-        load_x(1, 6)
         load_cos(7)
         load_x(0, 7)
         load_sin(7)
@@ -179,6 +181,9 @@ def tile_denseattentiononehead_pa_kernel(tc, hidden_states, W_q, cos, sin, out):
             return ap.rearrange("p (r u e) -> p r u e", u=2, e=2)
 
         def new_prod(i):
+            if i == 6:
+                tiles[i] = (t1d, t2d)
+                return
             t1n = prod.tile([P, B, 2, 512], F32, name="t1", tag="t1")
             t2n = prod.tile([P, B, 2, 512], F32, name="t2", tag="t2")
             tiles[i] = (t1n, t2n)
@@ -219,28 +224,31 @@ def tile_denseattentiononehead_pa_kernel(tc, hidden_states, W_q, cos, sin, out):
                 nc.tensor.matmul(out=xn[:, c], lhsT=identb[:], rhs=x_sb[b][:, i, c], start=True, stop=True)
             xbs[(i, b)] = xn
 
-        def weq(ap, w):
-            return ap.rearrange("p (w q e) -> p w e q", w=w, e=2)
+        def en(ap):
+            return ap.rearrange("p (n e) -> p e n", e=2)
 
-        def weq_out(ap, w):
-            return ap.rearrange("p (w e q) -> p w e q", w=w, e=2)
+        def en_out(ap):
+            return ap.rearrange("p (e n) -> p e n", e=2)
 
         def n_mul(i, b, k, eng, x):
             if i not in tiles:
                 new_prod(i)
             t1, t2 = tiles[i]
-            if k in (0, 2):
+            if k == 4:
+                eng.tensor_tensor(out=t1[:, b, :, :].rearrange("p g (e n) -> p g e n", e=2),
+                                  in0=x.rearrange("p (g n e) -> p g e n", g=2, e=2),
+                                  in1=cos_sb[:, i, :].rearrange("p (g n e) -> p g e n", g=2, e=2), op=MULT)
+            elif k in (0, 2):
                 c = slice(256 * k, 256 * k + 512)
-                eng.tensor_tensor(out=weq_out(t1[:, b, k // 2, :], 2), in0=weq(x[:, c], 2), in1=weq(cos_sb[:, i, c], 2), op=MULT)
+                eng.tensor_tensor(out=en_out(t1[:, b, k // 2, :]), in0=en(x[:, c]), in1=en(cos_sb[:, i, c]), op=MULT)
             elif k == 1:
-                eng.tensor_tensor(out=weq_out(t2[:, b, 1, :], 2),
-                                  in0=weq(x[:, 0:512], 2), in1=weq(sin_sb[:, i, 512:1024], 2), op=MULT)
+                eng.tensor_tensor(out=en_out(t2[:, b, 1, :]), in0=en(x[:, 0:512]), in1=en(sin_sb[:, i, 512:1024]), op=MULT)
             else:
-                for u in range(2):
-                    c = slice(256 * u, 256 * u + 256)
-                    eng.scalar_tensor_tensor(out=t2[:, b, 0, c].rearrange("p (e q) -> p e q", e=2),
-                                             in0=x[:, 512:1024][:, c].rearrange("p (q e) -> p e q", e=2), scalar=-1.0,
-                                             in1=sin_sb[:, i, c].rearrange("p (q e) -> p e q", e=2), op0=MULT, op1=MULT)
+                eng.scalar_tensor_tensor(out=en_out(t2[:, b, 0, :]), in0=en(x[:, 512:1024]), scalar=-1.0,
+                                         in1=en(sin_sb[:, i, 0:512]), op0=MULT, op1=MULT)
+
+        def c_mul(i, b, k):
+            n_mul(i, b, k, nc.gpsimd, x_sb[b][:, i, :])
 
         def d_mul(i, b, k):
             n_mul(i, b, k, nc.vector, xbs[(i, b)][:])
@@ -256,8 +264,10 @@ def tile_denseattentiononehead_pa_kernel(tc, hidden_states, W_q, cos, sin, out):
             hb = tp.tile([P, 512], F32, name="hb", tag="tp")
             for t in range(4):
                 c = slice(t * P, (t + 1) * P)
-                nc.tensor.matmul(out=hb[:, c], lhsT=t1[:, b, g, c], rhs=ident[:], is_transpose=True, start=True, stop=False)
-                nc.tensor.matmul(out=hb[:, c], lhsT=t2[:, b, g, c], rhs=ident[:], is_transpose=True, start=False, stop=True)
+                s0 = 256 * (t % 2) + P * (t // 2)
+                s = slice(s0, s0 + P)
+                nc.tensor.matmul(out=hb[:, c], lhsT=t1[:, b, g, s], rhs=ident[:], is_transpose=True, start=True, stop=False)
+                nc.tensor.matmul(out=hb[:, c], lhsT=t2[:, b, g, s], rhs=ident[:], is_transpose=True, start=False, stop=True)
             h_out = grps[i][:, b, g, :].rearrange("p (r t) -> p r t", t=4)
             h_in = hb[:].rearrange("p (t r) -> p r t", t=4)
             if v:
@@ -287,14 +297,11 @@ def tile_denseattentiononehead_pa_kernel(tc, hidden_states, W_q, cos, sin, out):
                     nc.tensor.transpose(
                         wb[:, u * 256 + oi * P:u * 256 + (oi + 1) * P],
                         src[:, (2 * g + u) * P:(2 * g + u + 1) * P], ident[:])
-            o0 = (512 * a + 256 * h) * 4
-            pairs_out(wg[:, g, o0:o0 + 1024], wb)
+            pairs_out(wg[:, a, g, 1024 * h:1024 * h + 1024], wb)
 
         def wq(a, g):
             nc.vector.quantize_mx(
-                out=wc[:, g, 512 * a:512 * a + 512].bitcast(FP8X4),
-                scales=ws[:, g, 512 * a:512 * a + 512],
-                in_=wg[:, g, 2048 * a:2048 * a + 2048])
+                out=wc[:, a, g, :].bitcast(FP8X4), scales=ws[:, a, g, :], in_=wg[:, a, g, :])
 
         def mx(i, b, nh, v=False):
             if (i, b) not in outs:
@@ -308,8 +315,8 @@ def tile_denseattentiononehead_pa_kernel(tc, hidden_states, W_q, cos, sin, out):
                     out=acc[:],
                     lhsT=hc[:, i, m0:m0 + P].bitcast(FP8X4),
                     lhsT_scale=hs[:, i, m0:m0 + P],
-                    rhs=wc[:, g, 512 * nh:512 * nh + 512].bitcast(FP8X4),
-                    rhs_scale=ws[:, g, 512 * nh:512 * nh + 512],
+                    rhs=wc[:, nh, g, :].bitcast(FP8X4),
+                    rhs_scale=ws[:, nh, g, :],
                     start=(g == 0), stop=(g == 1))
             if v:
                 nc.vector.tensor_copy(out=o_sb[:, 512 * nh:512 * nh + 512], in_=acc[:])
@@ -320,13 +327,13 @@ def tile_denseattentiononehead_pa_kernel(tc, hidden_states, W_q, cos, sin, out):
             c = slice(0, H) if nh is None else slice(512 * nh, 512 * nh + 512)
             nc.sync.dma_start(out=ov[:, b, i, c], in_=outs[(i, b)][:, c])
 
+        c_mul(6, 1, 4)
         s_mul(0, 0, 0)
         s_mul(0, 0, 1)
         s_mul(0, 0, 2)
         s_mul(0, 0, 3)
-        s_mul(0, 1, 0)
+        s_mul(0, 1, 4)
         s_mul(0, 1, 1)
-        s_mul(0, 1, 2)
         s_mul(0, 1, 3)
         cos_tr(1)
         x_t(1, 0)
@@ -338,6 +345,7 @@ def tile_denseattentiononehead_pa_kernel(tc, hidden_states, W_q, cos, sin, out):
         a_mul(1, 0, 1)
         a_mul(1, 1, 0)
         a_mul(1, 1, 1)
+        quant_b(0, 0)
         cos_tr(2)
         x_t(2, 0)
         sin_tr(2)
@@ -351,16 +359,15 @@ def tile_denseattentiononehead_pa_kernel(tc, hidden_states, W_q, cos, sin, out):
         a_mul(2, 1, 1)
         wtr(0, 0, 0)
         wtr(0, 0, 1)
+        x_t(3, 0)
         wtr(0, 1, 0)
         wtr(0, 1, 1)
-        cos_tr(3)
-        x_t(3, 0)
-        sin_tr(3)
         x_t(3, 1)
+        cos_tr(3)
+        sin_tr(3)
+        quant_b(0, 1)
         wq(0, 0)
         wq(0, 1)
-        quant_b(0, 0)
-        quant_b(0, 1)
         quant(1)
         add_all(2, nc.gpsimd)
         a_mul(3, 0, 0)
@@ -392,7 +399,7 @@ def tile_denseattentiononehead_pa_kernel(tc, hidden_states, W_q, cos, sin, out):
         d_x(6, 1)
         a_mul(4, 1, 0)
         a_mul(4, 1, 1)
-        d_mul(6, 1, 0)
+        d_mul(6, 1, 1)
         mx(0, 0, 1)
         store(0, 0)
         mx(0, 1, 1)
@@ -402,8 +409,6 @@ def tile_denseattentiononehead_pa_kernel(tc, hidden_states, W_q, cos, sin, out):
         sin_tr(5)
         quant(3)
         add_all(4, nc.gpsimd)
-        d_mul(6, 1, 1)
-        d_mul(6, 1, 2)
         d_mul(6, 1, 3)
         a_mul(5, 0, 0)
         a_mul(5, 0, 1)
@@ -430,9 +435,8 @@ def tile_denseattentiononehead_pa_kernel(tc, hidden_states, W_q, cos, sin, out):
         mx(3, 1, 1)
         store(3, 1)
         sin_tr(7)
-        d_mul(6, 0, 0)
+        d_mul(6, 0, 4)
         d_mul(6, 0, 1)
-        d_mul(6, 0, 2)
         d_mul(6, 0, 3)
         x_t(7, 0)
         a_mul(7, 0, 0)
@@ -445,10 +449,10 @@ def tile_denseattentiononehead_pa_kernel(tc, hidden_states, W_q, cos, sin, out):
         store(6, 1)
         p_add(6, 0, 1)
         p_add(6, 0, 0)
+        x_t(7, 1)
         mx(4, 1, 0)
         mx(4, 1, 1)
         store(4, 1)
-        x_t(7, 1)
         quant(5)
         quant_b(6, 0)
         add_b(7, 0, nc.gpsimd)

@@ -35,8 +35,7 @@ def tile_denseattentiononehead_pa_kernel(tc, hidden_states, W_q, cos, sin, out):
         dpool = ctx.enter_context(tc.tile_pool(name="dpool", bufs=2))
         opool = ctx.enter_context(tc.tile_pool(name="opool", bufs=5))
         px = ctx.enter_context(tc.psum_pool(name="px", bufs=3))
-        tp = ctx.enter_context(tc.psum_pool(name="tp", bufs=2))
-        pa = ctx.enter_context(tc.psum_pool(name="pa", bufs=3))
+        ps = ctx.enter_context(tc.psum_pool(name="ps", bufs=5))
         ctx.enter_context(tc.manual_schedule())
 
         x0_sb = res.tile([P, NT, H], BF16, name="x0_sb")
@@ -129,7 +128,7 @@ def tile_denseattentiononehead_pa_kernel(tc, hidden_states, W_q, cos, sin, out):
         load_x(1, 7)
         warm = res.tile([P, 512], BF16, name="warm")
         nc.vector.memset(warm[:], 0.0)
-        wacc = pa.tile([P, 512], F32, name="wacc", tag="acc")
+        wacc = ps.tile([P, 512], F32, name="wacc", tag="ps")
         for k in range(NWARM):
             nc.tensor.matmul(out=wacc[:], lhsT=warm[:, 0:P], rhs=warm[:], start=True, stop=True)
 
@@ -153,14 +152,14 @@ def tile_denseattentiononehead_pa_kernel(tc, hidden_states, W_q, cos, sin, out):
 
 
         def cos_tr(i):
-            cb = tp.tile([P, 512], F32, name="cb", tag="tp")
+            cb = ps.tile([P, 512], F32, name="cb", tag="ps")
             word_t(cb, cos_sb[:, i, :].bitcast(F32), False)
             cos_t = tabs.tile([P, H], BF16, name="cos_t", tag="cos_t")
             pairs_out(cos_t[:], cb)
             tab[(i, 0)] = cos_t
 
         def sin_tr(i):
-            sb = tp.tile([P, 512], F32, name="sb", tag="tp")
+            sb = ps.tile([P, 512], F32, name="sb", tag="ps")
             word_t(sb, sin_sb[:, i, :].bitcast(F32), True)
             sin_t = tabs.tile([P, H], BF16, name="sin_t", tag="sin_t")
             nc.scalar.copy(
@@ -261,7 +260,7 @@ def tile_denseattentiononehead_pa_kernel(tc, hidden_states, W_q, cos, sin, out):
                 grpd = dpool.tile([P, B, 2, 512], BF16, name="grpd", tag="grpd", align_bytes=64)
                 grps[i] = grpd
             t1, t2 = tiles[i]
-            hb = tp.tile([P, 512], F32, name="hb", tag="tp")
+            hb = ps.tile([P, 512], F32, name="hb", tag="ps")
             for t in range(4):
                 c = slice(t * P, (t + 1) * P)
                 s0 = 256 * (t % 2) + P * (t // 2)
@@ -290,7 +289,7 @@ def tile_denseattentiononehead_pa_kernel(tc, hidden_states, W_q, cos, sin, out):
                 in_=grps[i][:].rearrange("p b g c -> p (b g c)"))
 
         def wtr(a, g, h):
-            wb = tp.tile([P, 512], F32, name="wb", tag="tp")
+            wb = ps.tile([P, 512], F32, name="wb", tag="ps")
             for u in range(2):
                 for oi in range(2):
                     src = w_sb[:, 4 * a + 2 * h + oi, :].bitcast(F32)
@@ -308,7 +307,7 @@ def tile_denseattentiononehead_pa_kernel(tc, hidden_states, W_q, cos, sin, out):
                 o_new = opool.tile([P, H], F32, name="o_sb", tag="o_sb")
                 outs[(i, b)] = o_new
             o_sb = outs[(i, b)]
-            acc = pa.tile([P, 512], F32, name="acc", tag="acc")
+            acc = ps.tile([P, 512], F32, name="acc", tag="ps")
             for g in range(2):
                 m0 = (2 * b + g) * P
                 nc.tensor.matmul_mx(
@@ -359,12 +358,12 @@ def tile_denseattentiononehead_pa_kernel(tc, hidden_states, W_q, cos, sin, out):
         a_mul(2, 1, 1)
         wtr(0, 0, 0)
         wtr(0, 0, 1)
-        x_t(3, 0)
         wtr(0, 1, 0)
         wtr(0, 1, 1)
-        x_t(3, 1)
         cos_tr(3)
+        x_t(3, 0)
         sin_tr(3)
+        x_t(3, 1)
         quant_b(0, 1)
         wq(0, 0)
         wq(0, 1)
@@ -375,12 +374,12 @@ def tile_denseattentiononehead_pa_kernel(tc, hidden_states, W_q, cos, sin, out):
         a_mul(3, 1, 0)
         a_mul(3, 1, 1)
         wtr(1, 0, 0)
-        mx(1, 0, 0)
         wtr(1, 0, 1)
+        mx(1, 0, 0)
         mx(1, 1, 0)
         wtr(1, 1, 0)
-        mx(0, 0, 0)
         wtr(1, 1, 1)
+        mx(0, 0, 0)
         mx(0, 1, 0)
         cos_tr(4)
         x_t(4, 0)
@@ -396,14 +395,14 @@ def tile_denseattentiononehead_pa_kernel(tc, hidden_states, W_q, cos, sin, out):
         store(1, 0)
         mx(1, 1, 1)
         store(1, 1)
-        d_x(6, 1)
-        a_mul(4, 1, 0)
-        a_mul(4, 1, 1)
-        d_mul(6, 1, 1)
         mx(0, 0, 1)
         store(0, 0)
         mx(0, 1, 1)
         store(0, 1)
+        d_x(6, 1)
+        a_mul(4, 1, 0)
+        a_mul(4, 1, 1)
+        d_mul(6, 1, 1)
         cos_tr(5)
         x_t(5, 0)
         sin_tr(5)

from contextlib import ExitStack

import concourse.mybir as mybir
from concourse.masks import make_identity

FLOPS = 2 * 2048 * 1024 * 1024

F32 = mybir.dt.float32
BF16 = mybir.dt.bfloat16
U32 = mybir.dt.uint32
U8 = mybir.dt.uint8
FP8X4 = mybir.dt.float8_e4m3fn_x4
MULT = mybir.AluOpType.mult
ADD = mybir.AluOpType.add

P = 128
B = 2
H = 1024
NT = 8
NWARM = 5


def tile_denseattentiononehead_pa_kernel(tc, hidden_states, W_q, cos, sin, out):
    nc = tc.nc
    xv = hidden_states.rearrange("b (q t) j -> q b t j", t=NT)
    cv = cos.rearrange("(q t) j -> q t j", t=NT)
    sv = sin.rearrange("(q t) j -> q t j", t=NT)
    wv = W_q.rearrange("(t q) j -> q t j", q=P)
    ov = out.rearrange("b (q t) o -> q b t o", t=NT)
    with ExitStack() as ctx:
        res = ctx.enter_context(tc.tile_pool(name="res", bufs=1))
        prod = ctx.enter_context(tc.tile_pool(name="prod", bufs=3))
        tabs = ctx.enter_context(tc.tile_pool(name="tabs", bufs=2))
        gpool = ctx.enter_context(tc.tile_pool(name="gpool", bufs=1))
        dpool = ctx.enter_context(tc.tile_pool(name="dpool", bufs=2))
        opool = ctx.enter_context(tc.tile_pool(name="opool", bufs=5))
        px = ctx.enter_context(tc.psum_pool(name="px", bufs=3))
        ps = ctx.enter_context(tc.psum_pool(name="ps", bufs=5))
        ctx.enter_context(tc.manual_schedule())

        x0_sb = res.tile([P, NT, H], BF16, name="x0_sb")
        x1_sb = res.tile([P, NT, H], BF16, name="x1_sb")
        x_sb = [x0_sb, x1_sb]
        cos_sb = res.tile([P, NT, H], BF16, name="cos_sb")
        sin_sb = res.tile([P, NT, H], BF16, name="sin_sb")
        w_sb = res.tile([P, NT, H], BF16, name="w_sb")
        wg = res.tile([P, 2, 2, 2048], BF16, name="wg", align_bytes=64)
        wc = res.tile([P, 2, 2, 512], U32, name="wc", align_bytes=64)
        ws = res.tile([P, 2, 2, 512], U8, name="ws", align_bytes=64)
        hc = res.tile([P, NT, 512], U32, name="hc", align_bytes=64)
        hs = res.tile([P, NT, 512], U8, name="hs", align_bytes=64)
        t1d = res.tile([P, B, 2, 512], F32, name="t1d")
        t2d = res.tile([P, B, 2, 512], F32, name="t2d")
        ident = res.tile([P, P], F32, name="ident")
        identb = res.tile([P, P], BF16, name="identb")

        def load_cos(t0, t1=None):
            t1 = t1 or t0 + 1
            nc.sync.dma_start(out=cos_sb[:, t0:t1, :], in_=cv[:, t0:t1, :])

        def load_sin(t0, t1=None):
            t1 = t1 or t0 + 1
            nc.sync.dma_start(out=sin_sb[:, t0:t1, :], in_=sv[:, t0:t1, :])

        def load_x(b, t0, t1=None):
            t1 = t1 or t0 + 1
            nc.sync.dma_start(out=x_sb[b][:, t0:t1, :], in_=xv[:, b, t0:t1, :])

        def load_xh(b, i, g):
            c = slice(512 * g, 512 * g + 512)
            nc.sync.dma_start(out=x_sb[b][:, i, c], in_=xv[:, b, i, c])

        def load_cosh(i, g):
            c = slice(512 * g, 512 * g + 512)
            nc.sync.dma_start(out=cos_sb[:, i, c], in_=cv[:, i, c])

        def load_sinh(i, g):
            c = slice(512 * g, 512 * g + 512)
            nc.sync.dma_start(out=sin_sb[:, i, c], in_=sv[:, i, c])

        def load(t0, t1):
            load_cos(t0, t1)
            load_x(0, t0, t1)
            load_sin(t0, t1)
            load_x(1, t0, t1)

        def load_w(a):
            nc.sync.dma_start(out=w_sb[:, 4 * a:4 * a + 4, :], in_=wv[:, 4 * a:4 * a + 4, :])

        make_identity(nc, identb[:])
        make_identity(nc, ident[:])
        load_xh(0, 0, 0)
        load_cosh(0, 0)
        load_sinh(0, 1)
        load_xh(0, 0, 1)
        load_cosh(0, 1)
        load_sinh(0, 0)
        load_x(1, 0)
        load_cos(1)
        load_x(0, 1)
        load_sin(1)
        load_x(1, 1)
        load_cos(6)
        load_x(1, 6)
        load_cos(2)
        load_x(0, 2)
        load_sin(2)
        load_x(1, 2)
        load_w(0)
        load_cos(3)
        load_x(0, 3)
        load_sin(3)
        load_x(1, 3)
        load_w(1)
        load_cos(4)
        load_x(0, 4)
        load_sin(4)
        load_x(1, 4)
        load_cos(5)
        load_x(0, 5)
        load_sin(5)
        load_x(1, 5)
        load_x(0, 6)
        load_sin(6)
        load_cos(7)
        load_x(0, 7)
        load_sin(7)
        load_x(1, 7)
        warm = res.tile([P, 512], BF16, name="warm")
        nc.vector.memset(warm[:], 0.0)
        wacc = ps.tile([P, 512], F32, name="wacc", tag="ps")
        for k in range(NWARM):
            nc.tensor.matmul(out=wacc[:], lhsT=warm[:, 0:P], rhs=warm[:], start=True, stop=True)

        def word_t(dst, src, swap):
            for u in range(2):
                for g in range(2):
                    w = 2 * ((1 - g) if swap else g) + u
                    nc.tensor.transpose(dst[:, (2 * u + g) * P:(2 * u + g + 1) * P],
                                        src[:, w * P:(w + 1) * P], ident[:])

        def pairs_out(dst_bf16, bank):
            nc.scalar.copy(
                out=dst_bf16.bitcast(F32).rearrange("p (r u) -> p r u", u=2),
                in_=bank[:].rearrange("p (u r) -> p r u", u=2))

        tab = {}
        xbs = {}
        tiles = {}
        grps = {}
        outs = {}


        def cos_tr(i):
            cb = ps.tile([P, 512], F32, name="cb", tag="ps")
            word_t(cb, cos_sb[:, i, :].bitcast(F32), False)
            cos_t = tabs.tile([P, H], BF16, name="cos_t", tag="cos_t")
            pairs_out(cos_t[:], cb)
            tab[(i, 0)] = cos_t

        def sin_tr(i):
            sb = ps.tile([P, 512], F32, name="sb", tag="ps")
            word_t(sb, sin_sb[:, i, :].bitcast(F32), True)
            sin_t = tabs.tile([P, H], BF16, name="sin_t", tag="sin_t")
            nc.scalar.copy(
                out=sin_t[:, 0:512].bitcast(F32).rearrange("p (r u) -> p r u", u=2),
                in_=sb[:].rearrange("p (u g r) -> p g r u", u=2, g=2)[:, 0, :, :])
            nc.scalar.mul(
                out=sin_t[:, 512:1024].rearrange("p (r u e) -> p r u e", u=2, e=2),
                in_=sb[:].bitcast(BF16).rearrange("p (u g r e) -> p g r u e", u=2, g=2, e=2)[:, 1, :, :, :],
                mul=-1.0)
            tab[(i, 1)] = sin_t

        def x_t(i, b):
            xb = px.tile([P, 512], F32, name="xb", tag="xb")
            word_t(xb, x_sb[b][:, i, :].bitcast(F32), False)
            xbs[(i, b)] = xb

        def rue(ap):
            return ap.rearrange("p (r u e) -> p r u e", u=2, e=2)

        def new_prod(i):
            if i == 6:
                tiles[i] = (t1d, t2d)
                return
            t1n = prod.tile([P, B, 2, 512], F32, name="t1", tag="t1")
            t2n = prod.tile([P, B, 2, 512], F32, name="t2", tag="t2")
            tiles[i] = (t1n, t2n)

        def a_mul(i, b, k):
            if i not in tiles:
                new_prod(i)
            xin = xbs[(i, b)][:].bitcast(BF16).rearrange("p (u r e) -> p r u e", u=2, e=2)
            nc.vector.tensor_tensor(out=rue(tiles[i][k][:, b, :, :].rearrange("p g c -> p (g c)")), in0=xin, in1=rue(tab[(i, k)][:]), op=MULT)

        def grp_of(i):
            if i not in grps:
                grpn = gpool.tile([P, B, 2, 512], BF16, name="grp", tag="grp", align_bytes=64)
                grps[i] = grpn
            return grps[i]

        def add_all(i, eng):
            grp = grp_of(i)
            t1, t2 = tiles[i]
            eng.tensor_tensor(out=grp[:], in0=t1[:], in1=t2[:, :, ::-1, :], op=ADD)

        def add_b(i, b, eng):
            grp = grp_of(i)
            t1, t2 = tiles[i]
            eng.tensor_tensor(out=grp[:, b, :, :], in0=t1[:, b, :, :], in1=t2[:, b, ::-1, :], op=ADD)

        def t_all(i):
            cos_tr(i)
            x_t(i, 0)
            sin_tr(i)
            x_t(i, 1)


        def d_x(i, b):
            xn = px.tile([P, H], BF16, name="xn", tag="xb")
            for h in range(2):
                c = slice(512 * h, 512 * h + 512)
                nc.tensor.matmul(out=xn[:, c], lhsT=identb[:], rhs=x_sb[b][:, i, c], start=True, stop=True)
            xbs[(i, b)] = xn

        def en(ap):
            return ap.rearrange("p (n e) -> p e n", e=2)

        def en_out(ap):
            return ap.rearrange("p (e n) -> p e n", e=2)

        def n_mul(i, b, k, eng, x):
            if i not in tiles:
                new_prod(i)
            t1, t2 = tiles[i]
            if k == 4:
                eng.tensor_tensor(out=t1[:, b, :, :].rearrange("p g (e n) -> p g e n", e=2),
                                  in0=x.rearrange("p (g n e) -> p g e n", g=2, e=2),
                                  in1=cos_sb[:, i, :].rearrange("p (g n e) -> p g e n", g=2, e=2), op=MULT)
            elif k in (0, 2):
                c = slice(256 * k, 256 * k + 512)
                eng.tensor_tensor(out=en_out(t1[:, b, k // 2, :]), in0=en(x[:, c]), in1=en(cos_sb[:, i, c]), op=MULT)
            elif k == 1:
                eng.tensor_tensor(out=en_out(t2[:, b, 1, :]), in0=en(x[:, 0:512]), in1=en(sin_sb[:, i, 512:1024]), op=MULT)
            else:
                eng.scalar_tensor_tensor(out=en_out(t2[:, b, 0, :]), in0=en(x[:, 512:1024]), scalar=-1.0,
                                         in1=en(sin_sb[:, i, 0:512]), op0=MULT, op1=MULT)

        def c_mul(i, b, k):
            n_mul(i, b, k, nc.gpsimd, x_sb[b][:, i, :])

        def d_mul(i, b, k):
            n_mul(i, b, k, nc.vector, xbs[(i, b)][:])

        def s_mul(i, b, k):
            n_mul(i, b, k, nc.vector, x_sb[b][:, i, :])

        def p_add(i, b, g, v=False):
            if i not in grps:
                grpd = dpool.tile([P, B, 2, 512], BF16, name="grpd", tag="grpd", align_bytes=64)
                grps[i] = grpd
            t1, t2 = tiles[i]
            hb = ps.tile([P, 512], F32, name="hb", tag="ps")
            for t in range(4):
                c = slice(t * P, (t + 1) * P)
                s0 = 256 * (t % 2) + P * (t // 2)
                s = slice(s0, s0 + P)
                nc.tensor.matmul(out=hb[:, c], lhsT=t1[:, b, g, s], rhs=ident[:], is_transpose=True, start=True, stop=False)
                nc.tensor.matmul(out=hb[:, c], lhsT=t2[:, b, g, s], rhs=ident[:], is_transpose=True, start=False, stop=True)
            h_out = grps[i][:, b, g, :].rearrange("p (r t) -> p r t", t=4)
            h_in = hb[:].rearrange("p (t r) -> p r t", t=4)
            if v:
                nc.vector.tensor_copy(out=h_out, in_=h_in)
            else:
                nc.scalar.copy(
                    out=grps[i][:, b, g, :].rearrange("p (c i t) -> p c t i", i=4, t=4),
                    in_=hb[:].rearrange("p (t c i) -> p c t i", t=4, i=4))


        def quant_b(i, b):
            nc.vector.quantize_mx(
                out=hc[:, i, 256 * b:256 * b + 256].bitcast(FP8X4),
                scales=hs[:, i, 256 * b:256 * b + 256],
                in_=grps[i][:, b, :, :].rearrange("p g c -> p (g c)"))

        def quant(i):
            nc.vector.quantize_mx(
                out=hc[:, i, :].bitcast(FP8X4), scales=hs[:, i, :],
                in_=grps[i][:].rearrange("p b g c -> p (b g c)"))

        def wtr(a, g, h):
            wb = ps.tile([P, 512], F32, name="wb", tag="ps")
            for u in range(2):
                for oi in range(2):
                    src = w_sb[:, 4 * a + 2 * h + oi, :].bitcast(F32)
                    nc.tensor.transpose(
                        wb[:, u * 256 + oi * P:u * 256 + (oi + 1) * P],
                        src[:, (2 * g + u) * P:(2 * g + u + 1) * P], ident[:])
            pairs_out(wg[:, a, g, 1024 * h:1024 * h + 1024], wb)

        def wq(a, g):
            nc.vector.quantize_mx(
                out=wc[:, a, g, :].bitcast(FP8X4), scales=ws[:, a, g, :], in_=wg[:, a, g, :])

        def mx(i, b, nh, v=False):
            if (i, b) not in outs:
                o_new = opool.tile([P, H], F32, name="o_sb", tag="o_sb")
                outs[(i, b)] = o_new
            o_sb = outs[(i, b)]
            acc = ps.tile([P, 512], F32, name="acc", tag="ps")
            for g in range(2):
                m0 = (2 * b + g) * P
                nc.tensor.matmul_mx(
                    out=acc[:],
                    lhsT=hc[:, i, m0:m0 + P].bitcast(FP8X4),
                    lhsT_scale=hs[:, i, m0:m0 + P],
                    rhs=wc[:, nh, g, :].bitcast(FP8X4),
                    rhs_scale=ws[:, nh, g, :],
                    start=(g == 0), stop=(g == 1))
            if v:
                nc.vector.tensor_copy(out=o_sb[:, 512 * nh:512 * nh + 512], in_=acc[:])
            else:
                nc.scalar.copy(out=o_sb[:, 512 * nh:512 * nh + 512], in_=acc[:])

        def store(i, b, nh=None):
            c = slice(0, H) if nh is None else slice(512 * nh, 512 * nh + 512)
            nc.sync.dma_start(out=ov[:, b, i, c], in_=outs[(i, b)][:, c])

        c_mul(6, 1, 4)
        s_mul(0, 0, 0)
        s_mul(0, 0, 1)
        s_mul(0, 0, 2)
        s_mul(0, 0, 3)
        s_mul(0, 1, 4)
        s_mul(0, 1, 1)
        s_mul(0, 1, 3)
        cos_tr(1)
        x_t(1, 0)
        sin_tr(1)
        p_add(0, 0, 1)
        x_t(1, 1)
        p_add(0, 0, 0)
        a_mul(1, 0, 0)
        a_mul(1, 0, 1)
        a_mul(1, 1, 0)
        a_mul(1, 1, 1)
        quant_b(0, 0)
        cos_tr(2)
        x_t(2, 0)
        sin_tr(2)
        p_add(0, 1, 1)
        p_add(0, 1, 0)
        x_t(2, 1)
        add_all(1, nc.gpsimd)
        a_mul(2, 0, 0)
        a_mul(2, 0, 1)
        a_mul(2, 1, 0)
        a_mul(2, 1, 1)
        wtr(0, 0, 0)
        wtr(0, 0, 1)
        wtr(0, 1, 0)
        wtr(0, 1, 1)
        cos_tr(3)
        x_t(3, 0)
        sin_tr(3)
        x_t(3, 1)
        quant_b(0, 1)
        wq(0, 0)
        wq(0, 1)
        quant(1)
        add_all(2, nc.gpsimd)
        a_mul(3, 0, 0)
        a_mul(3, 0, 1)
        a_mul(3, 1, 0)
        a_mul(3, 1, 1)
        wtr(1, 0, 0)
        wtr(1, 0, 1)
        mx(1, 0, 0)
        mx(1, 1, 0)
        wtr(1, 1, 0)
        wtr(1, 1, 1)
        mx(0, 0, 0)
        mx(0, 1, 0)
        cos_tr(4)
        x_t(4, 0)
        sin_tr(4)
        x_t(4, 1)
        wq(1, 0)
        wq(1, 1)
        quant(2)
        add_all(3, nc.gpsimd)
        a_mul(4, 0, 0)
        a_mul(4, 0, 1)
        mx(1, 0, 1)
        store(1, 0)
        mx(1, 1, 1)
        store(1, 1)
        mx(0, 0, 1)
        store(0, 0)
        mx(0, 1, 1)
        store(0, 1)
        d_x(6, 1)
        a_mul(4, 1, 0)
        a_mul(4, 1, 1)
        d_mul(6, 1, 1)
        cos_tr(5)
        x_t(5, 0)
        sin_tr(5)
        quant(3)
        add_all(4, nc.gpsimd)
        d_mul(6, 1, 3)
        a_mul(5, 0, 0)
        a_mul(5, 0, 1)
        mx(2, 0, 0)
        mx(2, 0, 1)
        store(2, 0)
        x_t(5, 1)
        mx(2, 1, 0)
        mx(2, 1, 1)
        store(2, 1)
        p_add(6, 1, 1)
        p_add(6, 1, 0)
        a_mul(5, 1, 0)
        a_mul(5, 1, 1)
        quant(4)
        add_all(5, nc.gpsimd)
        quant_b(6, 1)
        mx(3, 0, 0)
        mx(3, 0, 1)
        store(3, 0)
        d_x(6, 0)
        cos_tr(7)
        mx(3, 1, 0)
        mx(3, 1, 1)
        store(3, 1)
        sin_tr(7)
        d_mul(6, 0, 4)
        d_mul(6, 0, 1)
        d_mul(6, 0, 3)
        x_t(7, 0)
        a_mul(7, 0, 0)
        a_mul(7, 0, 1)
        mx(4, 0, 0)
        mx(4, 0, 1)
        store(4, 0)
        mx(6, 1, 0)
        mx(6, 1, 1)
        store(6, 1)
        p_add(6, 0, 1)
        p_add(6, 0, 0)
        x_t(7, 1)
        mx(4, 1, 0)
        mx(4, 1, 1)
        store(4, 1)
        quant(5)
        quant_b(6, 0)
        add_b(7, 0, nc.gpsimd)
        a_mul(7, 1, 0)
        a_mul(7, 1, 1)
        mx(5, 0, 0)
        mx(5, 0, 1)
        store(5, 0)
        mx(5, 1, 0)
        mx(5, 1, 1)
        store(5, 1)
        mx(6, 0, 0)
        mx(6, 0, 1)
        store(6, 0)
        quant_b(7, 0)
        add_b(7, 1, nc.vector)
        quant_b(7, 1)
        mx(7, 0, 0)
        store(7, 0, 0)
        mx(7, 0, 1, True)
        store(7, 0, 1)
        mx(7, 1, 0)
        store(7, 1, 0)
        mx(7, 1, 1, True)
        store(7, 1, 1)
